import numpy as np
import ml_dtypes


def mxq(x, axis, fmt="e4m3"):
    dtype, down = {"e4m3": (ml_dtypes.float8_e4m3fn, 7), "e5m2": (ml_dtypes.float8_e5m2, 14)}[fmt]
    v = np.moveaxis(np.asarray(x, np.float32).astype(ml_dtypes.bfloat16).astype(np.float64), axis, -1)
    blocks = v.reshape(v.shape[:-1] + (-1, 32))
    amax = np.abs(blocks).max(-1, keepdims=True)
    byte = np.maximum(np.where(amax > 0, np.frexp(amax)[1] - 1 + 127, 0) - down, 1)
    scale = np.exp2(byte - 127.0)
    codes = (blocks / scale).astype(np.float32).astype(dtype).astype(np.float64)
    return np.moveaxis((codes * scale).reshape(v.shape), -1, axis)


WIDE = False


def mx_kscale(k):
    if not WIDE:
        return np.ones(k)
    levels = np.array([10, -10, 5, -5, 0])
    a = np.random.permutation(np.resize(levels, k // 512 * 4)).reshape(k // 512, 4)
    idx = np.arange(k)
    return np.exp2(a[idx // 512, idx % 128 // 32])


BF16 = ml_dtypes.bfloat16


def bf(x):
    return np.asarray(x, np.float32).astype(BF16)


def f64(x):
    return np.asarray(x).astype(np.float64)


B, D, F, P = 256, 1024, 2048, 1024
GAIN = 4.0 / np.sqrt(F)


def sigmoid(v):
    return 1.0 / (1.0 + np.exp(-v))


def setup_inputs():
    s = mx_kscale(D)
    return {
        "x": bf(np.random.standard_normal((B, D)) * s),
        "features": bf(np.random.standard_normal((F, D)) / np.sqrt(D) / s),
        "prototypes": bf(np.random.standard_normal((P, D)) * s),
        "alpha": bf((0.5 + 0.05 * np.random.standard_normal(1)) * GAIN),
        "beta": bf((0.3 + 0.03 * np.random.standard_normal(1)) * GAIN),
        "theta": bf((2.0 + 0.1 * np.random.standard_normal(1)) * GAIN),
    }


def reference(x, features, prototypes, alpha, beta, theta):
    fq = mxq(f64(features), 1, "e4m3")
    xf = mxq(f64(x), 1, "e4m3") @ fq.T
    pf = mxq(f64(prototypes), 1, "e4m3") @ fq.T
    sx = sigmoid(xf)
    sp = sigmoid(pf)
    ax = xf * sx
    bp = pf * sp
    axq = mxq(ax, 1, "e4m3")
    bpq = mxq(bp, 1, "e4m3")
    sxq = mxq(sx, 1, "e4m3")
    spq = mxq(sp, 1, "e4m3")
    common = axq @ bpq.T
    x_distinctive = ax.sum(axis=1, keepdims=True) - (axq @ spq.T)
    p_distinctive = bp.sum(axis=1)[None, :] - (sxq @ bpq.T)
    return f64(theta) * common - f64(alpha) * x_distinctive - f64(beta) * p_distinctive

@@ -1,0 +1,298 @@
+import concourse.mybir as mybir
+from concourse.masks import make_identity
+
+F32 = mybir.dt.float32
+BF16 = mybir.dt.bfloat16
+U32 = mybir.dt.uint32
+U8 = mybir.dt.uint8
+FP8X4 = mybir.dt.float8_e4m3fn_x4
+FUNC = mybir.ActivationFunctionType
+ALU = mybir.AluOpType
+
+P = 128
+PACK = 4
+K_PASS = P * PACK
+
+B, D, F, N_PROTO = 256, 1024, 2048, 1024
+D_PASSES = D // K_PASS
+F_PASSES = F // K_PASS
+WORD_TILES = D // 2 // P
+
+BLOCK = 256
+BLOCK_TILES = BLOCK // P
+N_BLOCKS = (B + N_PROTO) // BLOCK
+HALF = F_PASSES // 2
+
+THETA, ALPHA, BETA, NEG_ALPHA, NEG_BETA = 0, 1, 2, 3, 4
+
+FLOPS = 2 * (B + N_PROTO) * F * D + 3 * 2 * B * N_PROTO * F
+
+
+def tile_tverskylayer_pa_kernel(tc, x, features, prototypes, alpha, beta, theta, out):
+    nc = tc.nc
+    with (
+        tc.tile_pool(name="const", bufs=1) as const,
+        tc.tile_pool(name="raw", bufs=1) as raw,
+        tc.tile_pool(name="keep", bufs=1) as keep,
+        tc.tile_pool(name="grouped", bufs=2) as grouped_pool,
+        tc.tile_pool(name="silu", bufs=4) as silu_pool,
+        tc.tile_pool(name="stage", bufs=2) as stage,
+        tc.tile_pool(name="proto_mx", bufs=3) as proto_mx,
+        tc.psum_pool(name="work", bufs=5) as work,
+        tc.psum_pool(name="sums", bufs=1) as sums_pool,
+        tc.psum_pool(name="acc", bufs=2) as acc_pool,
+        tc.manual_schedule(),
+    ):
+        x_raw = raw.tile([P, BLOCK_TILES, D], BF16)
+        nc.sync.dma_start(out=x_raw[:], in_=x.rearrange("(r p) d -> p r d", p=P))
+        f_raw = []
+        for g in range(F_PASSES):
+            rows = raw.tile([P, PACK, D], BF16, name="f_raw%d" % g)
+            nc.sync.dma_start(
+                out=rows[:],
+                in_=features[g * K_PASS : (g + 1) * K_PASS, :].rearrange("(p t) d -> p t d", t=PACK),
+            )
+            f_raw.append(rows)
+        block_raw = [x_raw]
+        for j in range(1, N_BLOCKS):
+            rows = raw.tile([P, BLOCK_TILES, D], BF16, name="p_raw%d" % j)
+            nc.sync.dma_start(
+                out=rows[:],
+                in_=prototypes[(j - 1) * BLOCK : j * BLOCK, :].rearrange("(r p) d -> p r d", p=P),
+            )
+            block_raw.append(rows)
+
+        theta_bf = const.tile([P, 1], BF16)
+        alpha_bf = const.tile([P, 1], BF16)
+        beta_bf = const.tile([P, 1], BF16)
+        nc.scalar.dma_start(out=theta_bf[:], in_=theta.partition_broadcast(P))
+        nc.scalar.dma_start(out=alpha_bf[:], in_=alpha.partition_broadcast(P))
+        nc.scalar.dma_start(out=beta_bf[:], in_=beta.partition_broadcast(P))
+
+        ident = const.tile([P, P], F32)
+        make_identity(nc, ident[:])
+        ones = const.tile([P, P], F32)
+        nc.vector.memset(ones[:], 1.0)
+        warm = const.tile([P, 1], F32)
+        nc.scalar.activation(out=warm[:], in_=ones[:, 0:1], func=FUNC.Silu)
+
+        gains = const.tile([P, 5], F32)
+        x_bias = const.tile([P, BLOCK_TILES], F32)
+
+        def spread_gains():
+            nc.vector.tensor_copy(out=gains[:, THETA : THETA + 1], in_=theta_bf[:])
+            nc.vector.tensor_copy(out=gains[:, ALPHA : ALPHA + 1], in_=alpha_bf[:])
+            nc.vector.tensor_copy(out=gains[:, BETA : BETA + 1], in_=beta_bf[:])
+            nc.vector.tensor_scalar_mul(
+                out=gains[:, NEG_ALPHA : NEG_BETA + 1], in0=gains[:, ALPHA : BETA + 1], scalar1=-1.0
+            )
+
+        def turn_rows(rows, n_tiles, tag):
+            grouped = grouped_pool.tile([P, D_PASSES, n_tiles * P, PACK], BF16, tag=tag, align_bytes=64)
+            row_words = rows[:].bitcast(F32)
+            grouped_words = grouped[:].bitcast(F32)
+            for r in range(n_tiles):
+                turned = work.tile([P, WORD_TILES, P], F32, tag="work")
+                for w in range(WORD_TILES):
+                    nc.tensor.transpose(turned[:, w, :], row_words[:, r, w * P : (w + 1) * P], ident[:])
+                source = turned[:].rearrange("q (k u) i -> q k i u", u=2)
+                target = grouped_words[:, :, r * P : (r + 1) * P, :]
+                if r % 2 == 0:
+                    nc.scalar.copy(out=target, in_=source)
+                else:
+                    nc.vector.tensor_copy(out=target, in_=source)
+            return grouped
+
+        def quantise_rows(grouped, n_tiles, name):
+            codes = keep.tile([P, D_PASSES, n_tiles * P], U32, name=name + "_codes", align_bytes=64)
+            scales = keep.tile([P, D_PASSES, n_tiles * P], U8, name=name + "_scales", align_bytes=64)
+            for k in range(D_PASSES):
+                nc.vector.quantize_mx(
+                    out=codes[:, k, :].bitcast(FP8X4),
+                    scales=scales[:, k, :],
+                    in_=grouped[:, k, :, :].rearrange("q c f -> q (c f)"),
+                )
+            return codes, scales
+
+        f_mx = {}
+        block_mx = {}
+        silu = {}
+        tanh = {}
+
+        def first_contraction(j, half):
+            silu[j, half] = silu_pool.tile([P, HALF, PACK, BLOCK], F32, name="silu_v", tag="silu")
+            tanh[j, half] = stage.tile([P, HALF, PACK, BLOCK], F32, name="tanh_v", tag="tanh")
+            c_codes, c_scales = block_mx[j]
+            for gl in range(HALF):
+                f_codes, f_scales = f_mx[half * HALF + gl]
+                for pair in range(PACK // 2):
+                    v = work.tile([P, 2, BLOCK], F32, tag="work")
+                    for s in range(2):
+                        m_cols = slice((2 * pair + s) * P, (2 * pair + s + 1) * P)
+                        for k in range(D_PASSES):
+                            nc.tensor.matmul_mx(
+                                out=v[:, s, :],
+                                lhsT=f_codes[:, k, m_cols].bitcast(FP8X4),
+                                lhsT_scale=f_scales[:, k, m_cols],
+                                rhs=c_codes[:, k, :].bitcast(FP8X4),
+                                rhs_scale=c_scales[:, k, :],
+                                start=(k == 0),
+                                stop=(k == D_PASSES - 1),
+                            )
+                    ts = slice(2 * pair, 2 * pair + 2)
+                    nc.scalar.activation(out=silu[j, half][:, gl, ts, :], in_=v[:], func=FUNC.Silu)
+                    nc.scalar.activation(out=tanh[j, half][:, gl, ts, :], in_=v[:], func=FUNC.Tanh, scale=0.5)
+
+        prod_mx = {}
+        sig_mx = {}
+
+        def new_mx_pair(j, name):
+            pool = keep if j == 0 else proto_mx
+            codes = pool.tile([P, F_PASSES, BLOCK], U32, name=name + "_codes", align_bytes=64)
+            scales = pool.tile([P, F_PASSES, BLOCK], U8, name=name + "_scales", align_bytes=64)
+            return codes, scales
+
+        def round_and_quantise(j, half):
+            if half == 0:
+                prod_mx[j] = new_mx_pair(j, "prod")
+                sig_mx[j] = new_mx_pair(j, "sig")
+            passes = slice(half * HALF, (half + 1) * HALF)
+            prod_bf = stage.tile([P, HALF, BLOCK, PACK], BF16, align_bytes=64)
+            sig_bf = stage.tile([P, HALF, BLOCK, PACK], BF16, align_bytes=64)
+            nc.vector.tensor_copy(out=prod_bf[:], in_=silu[j, half][:].rearrange("p g t c -> p g c t"))
+            nc.vector.tensor_scalar(
+                out=sig_bf[:],
+                in0=tanh[j, half][:].rearrange("p g t c -> p g c t"),
+                scalar1=0.5,
+                scalar2=0.5,
+                op0=ALU.mult,
+                op1=ALU.add,
+            )
+            for rounded, (codes, scales) in ((prod_bf, prod_mx[j]), (sig_bf, sig_mx[j])):
+                nc.vector.quantize_mx(
+                    out=codes[:, passes, :].rearrange("p g c -> p (g c)").bitcast(FP8X4),
+                    scales=scales[:, passes, :].rearrange("p g c -> p (g c)"),
+                    in_=rounded[:].rearrange("p g c t -> p (g c t)"),
+                )
+
+        sums = {}
+        spread = {}
+
+        def add_up(j):
+            sums[j] = sums_pool.tile([P, 2 * BLOCK_TILES, P], F32, name="sums_bank", tag="sums")
+            for ct in range(BLOCK_TILES):
+                cols = slice(ct * P, (ct + 1) * P)
+                for g in range(F_PASSES):
+                    for t in range(PACK):
+                        nc.tensor.matmul(
+                            out=sums[j][:, ct, :],
+                            lhsT=silu[j, g // HALF][:, g % HALF, t, cols],
+                            rhs=ident[:],
+                            start=(g == 0 and t == 0),
+                            stop=(g == F_PASSES - 1 and t == PACK - 1),
+                            is_transpose=True,
+                        )
+            total = stage.tile([P, BLOCK_TILES], F32)
+            nc.vector.tensor_reduce(
+                out=total[:], in_=sums[j][:, 0:BLOCK_TILES, :], axis=mybir.AxisListType.X, op=ALU.add
+            )
+            if j == 0:
+                nc.vector.tensor_scalar_mul(
+                    out=x_bias[:], in0=total[:], scalar1=gains[:, NEG_ALPHA : NEG_ALPHA + 1]
+                )
+            else:
+                spread[j] = stage.tile([P, BLOCK_TILES, P], F32, name="spread_sum", tag="spread")
+                for ct in range(BLOCK_TILES):
+                    nc.vector.tensor_scalar(
+                        out=spread[j][:, ct, :],
+                        in0=ones[:],
+                        scalar1=total[:, ct : ct + 1],
+                        scalar2=gains[:, NEG_BETA : NEG_BETA + 1],
+                        op0=ALU.mult,
+                        op1=ALU.mult,
+                    )
+
+        result = {}
+
+        def start_result(j):
+            for ct in range(BLOCK_TILES):
+                nc.tensor.transpose(sums[j][:, BLOCK_TILES + ct, :], spread[j][:, ct, :], ident[:])
+            result[j] = stage.tile([P, BLOCK_TILES, BLOCK], F32, name="result", tag="result")
+            for bt in range(BLOCK_TILES):
+                nc.scalar.activation(
+                    out=result[j][:, bt, :],
+                    in_=sums[j][:, BLOCK_TILES:, :].rearrange("p a c -> p (a c)"),
+                    func=FUNC.Identity,
+                    bias=x_bias[:, bt : bt + 1],
+                    scale=1.0,
+                )
+
+        out_view = out.rearrange("(bt p) n -> p bt n", p=P)
+
+        def second_contraction(j):
+            terms = (
+                (prod_mx[0], prod_mx[j], THETA),
+                (prod_mx[0], sig_mx[j], ALPHA),
+                (sig_mx[0], prod_mx[j], BETA),
+            )
+            for (l_codes, l_scales), (r_codes, r_scales), gain in terms:
+                acc = acc_pool.tile([P, BLOCK_TILES, BLOCK], F32, tag="acc")
+                for bt in range(BLOCK_TILES):
+                    m_cols = slice(bt * P, (bt + 1) * P)
+                    for g in range(F_PASSES):
+                        nc.tensor.matmul_mx(
+                            out=acc[:, bt, :],
+                            lhsT=l_codes[:, g, m_cols].bitcast(FP8X4),
+                            lhsT_scale=l_scales[:, g, m_cols],
+                            rhs=r_codes[:, g, :].bitcast(FP8X4),
+                            rhs_scale=r_scales[:, g, :],
+                            start=(g == 0),
+                            stop=(g == F_PASSES - 1),
+                        )
+                nc.vector.scalar_tensor_tensor(
+                    out=result[j][:],
+                    in0=acc[:],
+                    scalar=gains[:, gain : gain + 1],
+                    in1=result[j][:],
+                    op0=ALU.mult,
+                    op1=ALU.add,
+                )
+            nc.sync.dma_start(out=out_view[:, :, (j - 1) * BLOCK : j * BLOCK], in_=result[j][:])
+
+        turned_x = turn_rows(x_raw, BLOCK_TILES, "grouped_block")
+        turned_f = turn_rows(f_raw[0], PACK, "grouped_f")
+        block_mx[0] = quantise_rows(turned_x, BLOCK_TILES, "block0")
+        turned_g = turn_rows(f_raw[1], PACK, "grouped_f")
+        f_mx[0] = quantise_rows(turned_f, PACK, "f0")
+        f_mx[1] = quantise_rows(turned_g, PACK, "f1")
+        spread_gains()
+        first_contraction(0, 0)
+        turned_f = turn_rows(f_raw[2], PACK, "grouped_f")
+        turned_g = turn_rows(f_raw[3], PACK, "grouped_f")
+        f_mx[2] = quantise_rows(turned_f, PACK, "f2")
+        turned_b = turn_rows(block_raw[1], BLOCK_TILES, "grouped_block")
+        f_mx[3] = quantise_rows(turned_g, PACK, "f3")
+        block_mx[1] = quantise_rows(turned_b, BLOCK_TILES, "block1")
+        first_contraction(0, 1)
+        round_and_quantise(0, 0)
+
+        for j in range(1, N_BLOCKS):
+            first_contraction(j, 0)
+            round_and_quantise(j - 1, 1)
+            add_up(j - 1)
+            if j + 1 < N_BLOCKS:
+                turned_b = turn_rows(block_raw[j + 1], BLOCK_TILES, "grouped_block")
+            if j > 1:
+                start_result(j - 1)
+            if j + 1 < N_BLOCKS:
+                block_mx[j + 1] = quantise_rows(turned_b, BLOCK_TILES, "block%d" % (j + 1))
+            first_contraction(j, 1)
+            round_and_quantise(j, 0)
+            if j > 1:
+                second_contraction(j - 1)
+
+        last = N_BLOCKS - 1
+        round_and_quantise(last, 1)
+        add_up(last)
+        start_result(last)
+        second_contraction(last)

@@ -21,7 +21,6 @@ WORD_TILES = D // 2 // P
 BLOCK = 256
 BLOCK_TILES = BLOCK // P
 N_BLOCKS = (B + N_PROTO) // BLOCK
-HALF = F_PASSES // 2
 
 THETA, ALPHA, BETA, NEG_ALPHA, NEG_BETA = 0, 1, 2, 3, 4
 
@@ -35,14 +34,20 @@ def tile_tverskylayer_pa_kernel(tc, x, features, prototypes, alpha, beta, theta,
         tc.tile_pool(name="raw", bufs=1) as raw,
         tc.tile_pool(name="keep", bufs=1) as keep,
         tc.tile_pool(name="grouped", bufs=2) as grouped_pool,
-        tc.tile_pool(name="silu", bufs=4) as silu_pool,
-        tc.tile_pool(name="stage", bufs=2) as stage,
+        tc.tile_pool(name="silu", bufs=2 * F_PASSES) as silu_pool,
+        tc.tile_pool(name="stage", bufs=3) as stage,
         tc.tile_pool(name="proto_mx", bufs=3) as proto_mx,
-        tc.psum_pool(name="work", bufs=5) as work,
+        tc.psum_pool(name="work", bufs=4) as work,
         tc.psum_pool(name="sums", bufs=1) as sums_pool,
-        tc.psum_pool(name="acc", bufs=2) as acc_pool,
+        tc.psum_pool(name="acc", bufs=3) as acc_pool,
         tc.manual_schedule(),
     ):
+        theta_bf = const.tile([P, 1], BF16)
+        alpha_bf = const.tile([P, 1], BF16)
+        beta_bf = const.tile([P, 1], BF16)
+        nc.scalar.dma_start(out=theta_bf[:], in_=theta.partition_broadcast(P))
+        nc.scalar.dma_start(out=alpha_bf[:], in_=alpha.partition_broadcast(P))
+        nc.scalar.dma_start(out=beta_bf[:], in_=beta.partition_broadcast(P))
         x_raw = raw.tile([P, BLOCK_TILES, D], BF16)
         nc.sync.dma_start(out=x_raw[:], in_=x.rearrange("(r p) d -> p r d", p=P))
         f_raw = []
@@ -61,13 +66,6 @@ def tile_tverskylayer_pa_kernel(tc, x, features, prototypes, alpha, beta, theta,
                 in_=prototypes[(j - 1) * BLOCK : j * BLOCK, :].rearrange("(r p) d -> p r d", p=P),
             )
             block_raw.append(rows)
-
-        theta_bf = const.tile([P, 1], BF16)
-        alpha_bf = const.tile([P, 1], BF16)
-        beta_bf = const.tile([P, 1], BF16)
-        nc.scalar.dma_start(out=theta_bf[:], in_=theta.partition_broadcast(P))
-        nc.scalar.dma_start(out=alpha_bf[:], in_=alpha.partition_broadcast(P))
-        nc.scalar.dma_start(out=beta_bf[:], in_=beta.partition_broadcast(P))
 
         ident = const.tile([P, P], F32)
         make_identity(nc, ident[:])
@@ -97,10 +95,10 @@ def tile_tverskylayer_pa_kernel(tc, x, features, prototypes, alpha, beta, theta,
                     nc.tensor.transpose(turned[:, w, :], row_words[:, r, w * P : (w + 1) * P], ident[:])
                 source = turned[:].rearrange("q (k u) i -> q k i u", u=2)
                 target = grouped_words[:, :, r * P : (r + 1) * P, :]
-                if r % 2 == 0:
-                    nc.scalar.copy(out=target, in_=source)
-                else:
+                if r % PACK == PACK - 1:
                     nc.vector.tensor_copy(out=target, in_=source)
+                else:
+                    nc.scalar.copy(out=target, in_=source)
             return grouped
 
         def quantise_rows(grouped, n_tiles, name):
@@ -119,29 +117,28 @@ def tile_tverskylayer_pa_kernel(tc, x, features, prototypes, alpha, beta, theta,
         silu = {}
         tanh = {}
 
-        def first_contraction(j, half):
-            silu[j, half] = silu_pool.tile([P, HALF, PACK, BLOCK], F32, name="silu_v", tag="silu")
-            tanh[j, half] = stage.tile([P, HALF, PACK, BLOCK], F32, name="tanh_v", tag="tanh")
+        def first_contraction(j, g):
+            silu[j, g] = silu_pool.tile([P, PACK, BLOCK], F32, name="silu_v", tag="silu")
+            tanh[j, g] = stage.tile([P, PACK, BLOCK], F32, name="tanh_v", tag="tanh")
             c_codes, c_scales = block_mx[j]
-            for gl in range(HALF):
-                f_codes, f_scales = f_mx[half * HALF + gl]
-                for pair in range(PACK // 2):
-                    v = work.tile([P, 2, BLOCK], F32, tag="work")
-                    for s in range(2):
-                        m_cols = slice((2 * pair + s) * P, (2 * pair + s + 1) * P)
-                        for k in range(D_PASSES):
-                            nc.tensor.matmul_mx(
-                                out=v[:, s, :],
-                                lhsT=f_codes[:, k, m_cols].bitcast(FP8X4),
-                                lhsT_scale=f_scales[:, k, m_cols],
-                                rhs=c_codes[:, k, :].bitcast(FP8X4),
-                                rhs_scale=c_scales[:, k, :],
-                                start=(k == 0),
-                                stop=(k == D_PASSES - 1),
-                            )
-                    ts = slice(2 * pair, 2 * pair + 2)
-                    nc.scalar.activation(out=silu[j, half][:, gl, ts, :], in_=v[:], func=FUNC.Silu)
-                    nc.scalar.activation(out=tanh[j, half][:, gl, ts, :], in_=v[:], func=FUNC.Tanh, scale=0.5)
+            f_codes, f_scales = f_mx[g]
+            for pair in range(PACK // 2):
+                v = work.tile([P, 2, BLOCK], F32, tag="work")
+                for s in range(2):
+                    m_cols = slice((2 * pair + s) * P, (2 * pair + s + 1) * P)
+                    for k in range(D_PASSES):
+                        nc.tensor.matmul_mx(
+                            out=v[:, s, :],
+                            lhsT=f_codes[:, k, m_cols].bitcast(FP8X4),
+                            lhsT_scale=f_scales[:, k, m_cols],
+                            rhs=c_codes[:, k, :].bitcast(FP8X4),
+                            rhs_scale=c_scales[:, k, :],
+                            start=(k == 0),
+                            stop=(k == D_PASSES - 1),
+                        )
+                ts = slice(2 * pair, 2 * pair + 2)
+                nc.scalar.activation(out=silu[j, g][:, ts, :], in_=v[:], func=FUNC.Silu)
+                nc.scalar.activation(out=tanh[j, g][:, ts, :], in_=v[:], func=FUNC.Tanh, scale=0.5)
 
         prod_mx = {}
         sig_mx = {}
@@ -152,17 +149,16 @@ def tile_tverskylayer_pa_kernel(tc, x, features, prototypes, alpha, beta, theta,
             scales = pool.tile([P, F_PASSES, BLOCK], U8, name=name + "_scales", align_bytes=64)
             return codes, scales
 
-        def round_and_quantise(j, half):
-            if half == 0:
+        def round_and_quantise(j, g):
+            if g == 0:
                 prod_mx[j] = new_mx_pair(j, "prod")
                 sig_mx[j] = new_mx_pair(j, "sig")
-            passes = slice(half * HALF, (half + 1) * HALF)
-            prod_bf = stage.tile([P, HALF, BLOCK, PACK], BF16, align_bytes=64)
-            sig_bf = stage.tile([P, HALF, BLOCK, PACK], BF16, align_bytes=64)
-            nc.vector.tensor_copy(out=prod_bf[:], in_=silu[j, half][:].rearrange("p g t c -> p g c t"))
+            prod_bf = stage.tile([P, BLOCK, PACK], BF16, align_bytes=64)
+            sig_bf = stage.tile([P, BLOCK, PACK], BF16, align_bytes=64)
+            nc.vector.tensor_copy(out=prod_bf[:], in_=silu[j, g][:].rearrange("p t c -> p c t"))
             nc.vector.tensor_scalar(
                 out=sig_bf[:],
-                in0=tanh[j, half][:].rearrange("p g t c -> p g c t"),
+                in0=tanh[j, g][:].rearrange("p t c -> p c t"),
                 scalar1=0.5,
                 scalar2=0.5,
                 op0=ALU.mult,
@@ -170,9 +166,9 @@ def tile_tverskylayer_pa_kernel(tc, x, features, prototypes, alpha, beta, theta,
             )
             for rounded, (codes, scales) in ((prod_bf, prod_mx[j]), (sig_bf, sig_mx[j])):
                 nc.vector.quantize_mx(
-                    out=codes[:, passes, :].rearrange("p g c -> p (g c)").bitcast(FP8X4),
-                    scales=scales[:, passes, :].rearrange("p g c -> p (g c)"),
-                    in_=rounded[:].rearrange("p g c t -> p (g c t)"),
+                    out=codes[:, g, :].bitcast(FP8X4),
+                    scales=scales[:, g, :],
+                    in_=rounded[:].rearrange("p c t -> p (c t)"),
                 )
 
         sums = {}
@@ -186,7 +182,7 @@ def tile_tverskylayer_pa_kernel(tc, x, features, prototypes, alpha, beta, theta,
                     for t in range(PACK):
                         nc.tensor.matmul(
                             out=sums[j][:, ct, :],
-                            lhsT=silu[j, g // HALF][:, g % HALF, t, cols],
+                            lhsT=silu[j, g][:, t, cols],
                             rhs=ident[:],
                             start=(g == 0 and t == 0),
                             stop=(g == F_PASSES - 1 and t == PACK - 1),
@@ -232,8 +228,8 @@ def tile_tverskylayer_pa_kernel(tc, x, features, prototypes, alpha, beta, theta,
         def second_contraction(j):
             terms = (
                 (prod_mx[0], prod_mx[j], THETA),
-                (prod_mx[0], sig_mx[j], ALPHA),
                 (sig_mx[0], prod_mx[j], BETA),
+                (prod_mx[0], sig_mx[j], ALPHA),
             )
             for (l_codes, l_scales), (r_codes, r_scales), gain in terms:
                 acc = acc_pool.tile([P, BLOCK_TILES, BLOCK], F32, tag="acc")
@@ -259,40 +255,40 @@ def tile_tverskylayer_pa_kernel(tc, x, features, prototypes, alpha, beta, theta,
                 )
             nc.sync.dma_start(out=out_view[:, :, (j - 1) * BLOCK : j * BLOCK], in_=result[j][:])
 
-        turned_x = turn_rows(x_raw, BLOCK_TILES, "grouped_block")
-        turned_f = turn_rows(f_raw[0], PACK, "grouped_f")
-        block_mx[0] = quantise_rows(turned_x, BLOCK_TILES, "block0")
-        turned_g = turn_rows(f_raw[1], PACK, "grouped_f")
-        f_mx[0] = quantise_rows(turned_f, PACK, "f0")
-        f_mx[1] = quantise_rows(turned_g, PACK, "f1")
+        turned = turn_rows(x_raw, BLOCK_TILES, "grouped_block")
+        block_mx[0] = quantise_rows(turned, BLOCK_TILES, "block0")
+        turned = turn_rows(f_raw[0], PACK, "grouped_f")
+        for g in range(F_PASSES):
+            f_mx[g] = quantise_rows(turned, PACK, "f%d" % g)
+            if g + 1 < F_PASSES:
+                turned = turn_rows(f_raw[g + 1], PACK, "grouped_f")
+            else:
+                turned = turn_rows(block_raw[1], BLOCK_TILES, "grouped_block")
+            first_contraction(0, g)
+            if g > 0:
+                round_and_quantise(0, g - 1)
+        block_mx[1] = quantise_rows(turned, BLOCK_TILES, "block1")
         spread_gains()
-        first_contraction(0, 0)
-        turned_f = turn_rows(f_raw[2], PACK, "grouped_f")
-        turned_g = turn_rows(f_raw[3], PACK, "grouped_f")
-        f_mx[2] = quantise_rows(turned_f, PACK, "f2")
-        turned_b = turn_rows(block_raw[1], BLOCK_TILES, "grouped_block")
-        f_mx[3] = quantise_rows(turned_g, PACK, "f3")
-        block_mx[1] = quantise_rows(turned_b, BLOCK_TILES, "block1")
-        first_contraction(0, 1)
-        round_and_quantise(0, 0)
 
         for j in range(1, N_BLOCKS):
             first_contraction(j, 0)
-            round_and_quantise(j - 1, 1)
-            add_up(j - 1)
-            if j + 1 < N_BLOCKS:
-                turned_b = turn_rows(block_raw[j + 1], BLOCK_TILES, "grouped_block")
-            if j > 1:
-                start_result(j - 1)
-            if j + 1 < N_BLOCKS:
-                block_mx[j + 1] = quantise_rows(turned_b, BLOCK_TILES, "block%d" % (j + 1))
+            round_and_quantise(j - 1, 3)
             first_contraction(j, 1)
             round_and_quantise(j, 0)
+            add_up(j - 1)
+            if j + 1 < N_BLOCKS:
+                turned = turn_rows(block_raw[j + 1], BLOCK_TILES, "grouped_block")
+                block_mx[j + 1] = quantise_rows(turned, BLOCK_TILES, "block%d" % (j + 1))
+            first_contraction(j, 2)
+            round_and_quantise(j, 1)
+            first_contraction(j, 3)
+            round_and_quantise(j, 2)
             if j > 1:
+                start_result(j - 1)
                 second_contraction(j - 1)
 
         last = N_BLOCKS - 1
-        round_and_quantise(last, 1)
+        round_and_quantise(last, 3)
         add_up(last)
         start_result(last)
         second_contraction(last)

@@ -21,6 +21,7 @@ WORD_TILES = D // 2 // P
 BLOCK = 256
 BLOCK_TILES = BLOCK // P
 N_BLOCKS = (B + N_PROTO) // BLOCK
+RUN = 4
 
 THETA, ALPHA, BETA, NEG_ALPHA, NEG_BETA = 0, 1, 2, 3, 4
 
@@ -155,10 +156,13 @@ def tile_tverskylayer_pa_kernel(tc, x, features, prototypes, alpha, beta, theta,
                 sig_mx[j] = new_mx_pair(j, "sig")
             prod_bf = stage.tile([P, BLOCK, PACK], BF16, align_bytes=64)
             sig_bf = stage.tile([P, BLOCK, PACK], BF16, align_bytes=64)
-            nc.vector.tensor_copy(out=prod_bf[:], in_=silu[j, g][:].rearrange("p t c -> p c t"))
+            nc.vector.tensor_copy(
+                out=prod_bf[:].rearrange("p (c i) t -> p c t i", i=RUN),
+                in_=silu[j, g][:].rearrange("p t (c i) -> p c t i", i=RUN),
+            )
             nc.vector.tensor_scalar(
-                out=sig_bf[:],
-                in0=tanh[j, g][:].rearrange("p t c -> p c t"),
+                out=sig_bf[:].rearrange("p (c i) t -> p c t i", i=RUN),
+                in0=tanh[j, g][:].rearrange("p t (c i) -> p c t i", i=RUN),
                 scalar1=0.5,
                 scalar2=0.5,
                 op0=ALU.mult,

@@ -41,7 +41,6 @@ def tile_tverskylayer_pa_kernel(tc, x, features, prototypes, alpha, beta, theta,
         tc.psum_pool(name="work", bufs=4) as work,
         tc.psum_pool(name="sums", bufs=1) as sums_pool,
         tc.psum_pool(name="acc", bufs=3) as acc_pool,
-        tc.manual_schedule(),
     ):
         theta_bf = const.tile([P, 1], BF16)
         alpha_bf = const.tile([P, 1], BF16)

@@ -35,7 +35,7 @@ def tile_tverskylayer_pa_kernel(tc, x, features, prototypes, alpha, beta, theta,
         tc.tile_pool(name="raw", bufs=1) as raw,
         tc.tile_pool(name="keep", bufs=1) as keep,
         tc.tile_pool(name="grouped", bufs=2) as grouped_pool,
-        tc.tile_pool(name="silu", bufs=2 * F_PASSES) as silu_pool,
+        tc.tile_pool(name="halved", bufs=2 * F_PASSES) as halved_pool,
         tc.tile_pool(name="stage", bufs=3) as stage,
         tc.tile_pool(name="proto_mx", bufs=3) as proto_mx,
         tc.psum_pool(name="work", bufs=4) as work,
@@ -118,7 +118,7 @@ def tile_tverskylayer_pa_kernel(tc, x, features, prototypes, alpha, beta, theta,
         tanh = {}
 
         def first_contraction(j, g):
-            silu[j, g] = silu_pool.tile([P, PACK, BLOCK], F32, name="silu_v", tag="silu")
+            silu[j, g] = stage.tile([P, PACK, BLOCK], F32, name="silu_v", tag="silu")
             tanh[j, g] = stage.tile([P, PACK, BLOCK], F32, name="tanh_v", tag="tanh")
             c_codes, c_scales = block_mx[j]
             f_codes, f_scales = f_mx[g]
@@ -140,6 +140,7 @@ def tile_tverskylayer_pa_kernel(tc, x, features, prototypes, alpha, beta, theta,
                 nc.scalar.activation(out=silu[j, g][:, ts, :], in_=v[:], func=FUNC.Silu)
                 nc.scalar.activation(out=tanh[j, g][:, ts, :], in_=v[:], func=FUNC.Tanh, scale=0.5)
 
+        halved = {}
         prod_mx = {}
         sig_mx = {}
 
@@ -167,6 +168,13 @@ def tile_tverskylayer_pa_kernel(tc, x, features, prototypes, alpha, beta, theta,
                 op0=ALU.mult,
                 op1=ALU.add,
             )
+            halved[j, g] = halved_pool.tile([P, PACK // 2, BLOCK], F32, name="halved_v", tag="halved")
+            nc.gpsimd.tensor_tensor(
+                out=halved[j, g][:],
+                in0=silu[j, g][:, 0 : PACK // 2, :],
+                in1=silu[j, g][:, PACK // 2 : PACK, :],
+                op=ALU.add,
+            )
             for rounded, (codes, scales) in ((prod_bf, prod_mx[j]), (sig_bf, sig_mx[j])):
                 nc.vector.quantize_mx(
                     out=codes[:, g, :].bitcast(FP8X4),
@@ -182,13 +190,13 @@ def tile_tverskylayer_pa_kernel(tc, x, features, prototypes, alpha, beta, theta,
             for ct in range(BLOCK_TILES):
                 cols = slice(ct * P, (ct + 1) * P)
                 for g in range(F_PASSES):
-                    for t in range(PACK):
+                    for t in range(PACK // 2):
                         nc.tensor.matmul(
                             out=sums[j][:, ct, :],
-                            lhsT=silu[j, g][:, t, cols],
+                            lhsT=halved[j, g][:, t, cols],
                             rhs=ident[:],
                             start=(g == 0 and t == 0),
-                            stop=(g == F_PASSES - 1 and t == PACK - 1),
+                            stop=(g == F_PASSES - 1 and t == PACK // 2 - 1),
                             is_transpose=True,
                         )
             total = stage.tile([P, BLOCK_TILES], F32)

@@ -22,6 +22,7 @@ BLOCK = 256
 BLOCK_TILES = BLOCK // P
 N_BLOCKS = (B + N_PROTO) // BLOCK
 RUN = 4
+PROD, SIG = 0, 1
 
 THETA, ALPHA, BETA, NEG_ALPHA, NEG_BETA = 0, 1, 2, 3, 4
 
@@ -35,7 +36,7 @@ def tile_tverskylayer_pa_kernel(tc, x, features, prototypes, alpha, beta, theta,
         tc.tile_pool(name="raw", bufs=1) as raw,
         tc.tile_pool(name="keep", bufs=1) as keep,
         tc.tile_pool(name="grouped", bufs=2) as grouped_pool,
-        tc.tile_pool(name="halved", bufs=2 * F_PASSES) as halved_pool,
+        tc.tile_pool(name="silu", bufs=2 * F_PASSES) as silu_pool,
         tc.tile_pool(name="stage", bufs=3) as stage,
         tc.tile_pool(name="proto_mx", bufs=3) as proto_mx,
         tc.psum_pool(name="work", bufs=4) as work,
@@ -104,12 +105,11 @@ def tile_tverskylayer_pa_kernel(tc, x, features, prototypes, alpha, beta, theta,
         def quantise_rows(grouped, n_tiles, name):
             codes = keep.tile([P, D_PASSES, n_tiles * P], U32, name=name + "_codes", align_bytes=64)
             scales = keep.tile([P, D_PASSES, n_tiles * P], U8, name=name + "_scales", align_bytes=64)
-            for k in range(D_PASSES):
-                nc.vector.quantize_mx(
-                    out=codes[:, k, :].bitcast(FP8X4),
-                    scales=scales[:, k, :],
-                    in_=grouped[:, k, :, :].rearrange("q c f -> q (c f)"),
-                )
+            nc.vector.quantize_mx(
+                out=codes[:].rearrange("q k c -> q (k c)").bitcast(FP8X4),
+                scales=scales[:].rearrange("q k c -> q (k c)"),
+                in_=grouped[:].rearrange("q k c f -> q (k c f)"),
+            )
             return codes, scales
 
         f_mx = {}
@@ -118,7 +118,7 @@ def tile_tverskylayer_pa_kernel(tc, x, features, prototypes, alpha, beta, theta,
         tanh = {}
 
         def first_contraction(j, g):
-            silu[j, g] = stage.tile([P, PACK, BLOCK], F32, name="silu_v", tag="silu")
+            silu[j, g] = silu_pool.tile([P, PACK, BLOCK], F32, name="silu_v", tag="silu")
             tanh[j, g] = stage.tile([P, PACK, BLOCK], F32, name="tanh_v", tag="tanh")
             c_codes, c_scales = block_mx[j]
             f_codes, f_scales = f_mx[g]
@@ -140,47 +140,33 @@ def tile_tverskylayer_pa_kernel(tc, x, features, prototypes, alpha, beta, theta,
                 nc.scalar.activation(out=silu[j, g][:, ts, :], in_=v[:], func=FUNC.Silu)
                 nc.scalar.activation(out=tanh[j, g][:, ts, :], in_=v[:], func=FUNC.Tanh, scale=0.5)
 
-        halved = {}
-        prod_mx = {}
-        sig_mx = {}
-
-        def new_mx_pair(j, name):
-            pool = keep if j == 0 else proto_mx
-            codes = pool.tile([P, F_PASSES, BLOCK], U32, name=name + "_codes", align_bytes=64)
-            scales = pool.tile([P, F_PASSES, BLOCK], U8, name=name + "_scales", align_bytes=64)
-            return codes, scales
+        second_mx = {}
 
         def round_and_quantise(j, g):
             if g == 0:
-                prod_mx[j] = new_mx_pair(j, "prod")
-                sig_mx[j] = new_mx_pair(j, "sig")
-            prod_bf = stage.tile([P, BLOCK, PACK], BF16, align_bytes=64)
-            sig_bf = stage.tile([P, BLOCK, PACK], BF16, align_bytes=64)
+                pool = keep if j == 0 else proto_mx
+                codes = pool.tile([P, F_PASSES, 2, BLOCK], U32, name="second_codes", align_bytes=64)
+                scales = pool.tile([P, F_PASSES, 2, BLOCK], U8, name="second_scales", align_bytes=64)
+                second_mx[j] = (codes, scales)
+            codes, scales = second_mx[j]
+            rounded = stage.tile([P, 2, BLOCK, PACK], BF16, align_bytes=64)
             nc.vector.tensor_copy(
-                out=prod_bf[:].rearrange("p (c i) t -> p c t i", i=RUN),
+                out=rounded[:, PROD, :, :].rearrange("p (c i) t -> p c t i", i=RUN),
                 in_=silu[j, g][:].rearrange("p t (c i) -> p c t i", i=RUN),
             )
             nc.vector.tensor_scalar(
-                out=sig_bf[:].rearrange("p (c i) t -> p c t i", i=RUN),
+                out=rounded[:, SIG, :, :].rearrange("p (c i) t -> p c t i", i=RUN),
                 in0=tanh[j, g][:].rearrange("p t (c i) -> p c t i", i=RUN),
                 scalar1=0.5,
                 scalar2=0.5,
                 op0=ALU.mult,
                 op1=ALU.add,
             )
-            halved[j, g] = halved_pool.tile([P, PACK // 2, BLOCK], F32, name="halved_v", tag="halved")
-            nc.gpsimd.tensor_tensor(
-                out=halved[j, g][:],
-                in0=silu[j, g][:, 0 : PACK // 2, :],
-                in1=silu[j, g][:, PACK // 2 : PACK, :],
-                op=ALU.add,
+            nc.vector.quantize_mx(
+                out=codes[:, g, :, :].rearrange("p k c -> p (k c)").bitcast(FP8X4),
+                scales=scales[:, g, :, :].rearrange("p k c -> p (k c)"),
+                in_=rounded[:].rearrange("p k c t -> p (k c t)"),
             )
-            for rounded, (codes, scales) in ((prod_bf, prod_mx[j]), (sig_bf, sig_mx[j])):
-                nc.vector.quantize_mx(
-                    out=codes[:, g, :].bitcast(FP8X4),
-                    scales=scales[:, g, :],
-                    in_=rounded[:].rearrange("p c t -> p (c t)"),
-                )
 
         sums = {}
         spread = {}
@@ -190,13 +176,13 @@ def tile_tverskylayer_pa_kernel(tc, x, features, prototypes, alpha, beta, theta,
             for ct in range(BLOCK_TILES):
                 cols = slice(ct * P, (ct + 1) * P)
                 for g in range(F_PASSES):
-                    for t in range(PACK // 2):
+                    for t in range(PACK):
                         nc.tensor.matmul(
                             out=sums[j][:, ct, :],
-                            lhsT=halved[j, g][:, t, cols],
+                            lhsT=silu[j, g][:, t, cols],
                             rhs=ident[:],
                             start=(g == 0 and t == 0),
-                            stop=(g == F_PASSES - 1 and t == PACK // 2 - 1),
+                            stop=(g == F_PASSES - 1 and t == PACK - 1),
                             is_transpose=True,
                         )
             total = stage.tile([P, BLOCK_TILES], F32)
@@ -237,22 +223,19 @@ def tile_tverskylayer_pa_kernel(tc, x, features, prototypes, alpha, beta, theta,
         out_view = out.rearrange("(bt p) n -> p bt n", p=P)
 
         def second_contraction(j):
-            terms = (
-                (prod_mx[0], prod_mx[j], THETA),
-                (sig_mx[0], prod_mx[j], BETA),
-                (prod_mx[0], sig_mx[j], ALPHA),
-            )
-            for (l_codes, l_scales), (r_codes, r_scales), gain in terms:
+            l_codes, l_scales = second_mx[0]
+            r_codes, r_scales = second_mx[j]
+            for x_kind, proto_kind, gain in ((PROD, PROD, THETA), (SIG, PROD, BETA), (PROD, SIG, ALPHA)):
                 acc = acc_pool.tile([P, BLOCK_TILES, BLOCK], F32, tag="acc")
                 for bt in range(BLOCK_TILES):
                     m_cols = slice(bt * P, (bt + 1) * P)
                     for g in range(F_PASSES):
                         nc.tensor.matmul_mx(
                             out=acc[:, bt, :],
-                            lhsT=l_codes[:, g, m_cols].bitcast(FP8X4),
-                            lhsT_scale=l_scales[:, g, m_cols],
-                            rhs=r_codes[:, g, :].bitcast(FP8X4),
-                            rhs_scale=r_scales[:, g, :],
+                            lhsT=l_codes[:, g, x_kind, m_cols].bitcast(FP8X4),
+                            lhsT_scale=l_scales[:, g, x_kind, m_cols],
+                            rhs=r_codes[:, g, proto_kind, :].bitcast(FP8X4),
+                            rhs_scale=r_scales[:, g, proto_kind, :],
                             start=(g == 0),
                             stop=(g == F_PASSES - 1),
                         )

@@ -46,9 +46,6 @@ def tile_tverskylayer_pa_kernel(tc, x, features, prototypes, alpha, beta, theta,
         theta_bf = const.tile([P, 1], BF16)
         alpha_bf = const.tile([P, 1], BF16)
         beta_bf = const.tile([P, 1], BF16)
-        nc.scalar.dma_start(out=theta_bf[:], in_=theta.partition_broadcast(P))
-        nc.scalar.dma_start(out=alpha_bf[:], in_=alpha.partition_broadcast(P))
-        nc.scalar.dma_start(out=beta_bf[:], in_=beta.partition_broadcast(P))
         x_raw = raw.tile([P, BLOCK_TILES, D], BF16)
         nc.sync.dma_start(out=x_raw[:], in_=x.rearrange("(r p) d -> p r d", p=P))
         f_raw = []
@@ -67,6 +64,9 @@ def tile_tverskylayer_pa_kernel(tc, x, features, prototypes, alpha, beta, theta,
                 in_=prototypes[(j - 1) * BLOCK : j * BLOCK, :].rearrange("(r p) d -> p r d", p=P),
             )
             block_raw.append(rows)
+        nc.sync.dma_start(out=theta_bf[:], in_=theta.partition_broadcast(P))
+        nc.sync.dma_start(out=alpha_bf[:], in_=alpha.partition_broadcast(P))
+        nc.sync.dma_start(out=beta_bf[:], in_=beta.partition_broadcast(P))
 
         ident = const.tile([P, P], F32)
         make_identity(nc, ident[:])

@@ -22,6 +22,7 @@ BLOCK = 256
 BLOCK_TILES = BLOCK // P
 N_BLOCKS = (B + N_PROTO) // BLOCK
 RUN = 4
+SCALAR, VECTOR = 0, 1
 PROD, SIG = 0, 1
 
 THETA, ALPHA, BETA, NEG_ALPHA, NEG_BETA = 0, 1, 2, 3, 4
@@ -35,9 +36,9 @@ def tile_tverskylayer_pa_kernel(tc, x, features, prototypes, alpha, beta, theta,
         tc.tile_pool(name="const", bufs=1) as const,
         tc.tile_pool(name="raw", bufs=1) as raw,
         tc.tile_pool(name="keep", bufs=1) as keep,
-        tc.tile_pool(name="grouped", bufs=2) as grouped_pool,
-        tc.tile_pool(name="silu", bufs=2 * F_PASSES) as silu_pool,
-        tc.tile_pool(name="stage", bufs=3) as stage,
+        tc.tile_pool(name="grouped", bufs=4) as grouped_pool,
+        tc.tile_pool(name="silu", bufs=10) as silu_pool,
+        tc.tile_pool(name="stage", bufs=4) as stage,
         tc.tile_pool(name="proto_mx", bufs=3) as proto_mx,
         tc.psum_pool(name="work", bufs=4) as work,
         tc.psum_pool(name="sums", bufs=1) as sums_pool,
@@ -46,24 +47,26 @@ def tile_tverskylayer_pa_kernel(tc, x, features, prototypes, alpha, beta, theta,
         theta_bf = const.tile([P, 1], BF16)
         alpha_bf = const.tile([P, 1], BF16)
         beta_bf = const.tile([P, 1], BF16)
-        x_raw = raw.tile([P, BLOCK_TILES, D], BF16)
-        nc.sync.dma_start(out=x_raw[:], in_=x.rearrange("(r p) d -> p r d", p=P))
-        f_raw = []
-        for g in range(F_PASSES):
-            rows = raw.tile([P, PACK, D], BF16, name="f_raw%d" % g)
-            nc.sync.dma_start(
-                out=rows[:],
-                in_=features[g * K_PASS : (g + 1) * K_PASS, :].rearrange("(p t) d -> p t d", t=PACK),
-            )
-            f_raw.append(rows)
-        block_raw = [x_raw]
-        for j in range(1, N_BLOCKS):
-            rows = raw.tile([P, BLOCK_TILES, D], BF16, name="p_raw%d" % j)
-            nc.sync.dma_start(
-                out=rows[:],
-                in_=prototypes[(j - 1) * BLOCK : j * BLOCK, :].rearrange("(r p) d -> p r d", p=P),
-            )
-            block_raw.append(rows)
+        def load_rows(name, source, tile_by_tile=False):
+            rows = raw.tile([P, BLOCK_TILES, D], BF16, name=name)
+            if tile_by_tile:
+                for r in range(BLOCK_TILES):
+                    nc.sync.dma_start(out=rows[:, r, :], in_=source[:, r, :])
+            else:
+                nc.sync.dma_start(out=rows[:], in_=source)
+            return rows
+
+        f_source = features.rearrange("(g p pair s) d -> g pair p s d", g=F_PASSES, p=P, pair=2)
+        p_source = prototypes.rearrange("(j r p) d -> j p r d", r=BLOCK_TILES, p=P)
+        units = [(g, pair) for g in range(F_PASSES) for pair in range(2)]
+        block_raw = {0: load_rows("x_raw", x.rearrange("(r p) d -> p r d", p=P), tile_by_tile=True)}
+        f_raw = {}
+        for i, (g, pair) in enumerate(units):
+            if i == 6:
+                block_raw[1] = load_rows("p_raw1", p_source[0])
+            f_raw[g, pair] = load_rows("f_raw%d_%d" % (g, pair), f_source[g, pair], tile_by_tile=(i == 0))
+        for j in range(2, N_BLOCKS):
+            block_raw[j] = load_rows("p_raw%d" % j, p_source[j - 1])
         nc.sync.dma_start(out=theta_bf[:], in_=theta.partition_broadcast(P))
         nc.sync.dma_start(out=alpha_bf[:], in_=alpha.partition_broadcast(P))
         nc.sync.dma_start(out=beta_bf[:], in_=beta.partition_broadcast(P))
@@ -86,25 +89,25 @@ def tile_tverskylayer_pa_kernel(tc, x, features, prototypes, alpha, beta, theta,
                 out=gains[:, NEG_ALPHA : NEG_BETA + 1], in0=gains[:, ALPHA : BETA + 1], scalar1=-1.0
             )
 
-        def turn_rows(rows, n_tiles, tag):
-            grouped = grouped_pool.tile([P, D_PASSES, n_tiles * P, PACK], BF16, tag=tag, align_bytes=64)
+        def turn_rows(rows, copy_engines):
+            grouped = grouped_pool.tile([P, D_PASSES, BLOCK, PACK], BF16, align_bytes=64)
             row_words = rows[:].bitcast(F32)
             grouped_words = grouped[:].bitcast(F32)
-            for r in range(n_tiles):
+            for r in range(BLOCK_TILES):
                 turned = work.tile([P, WORD_TILES, P], F32, tag="work")
                 for w in range(WORD_TILES):
                     nc.tensor.transpose(turned[:, w, :], row_words[:, r, w * P : (w + 1) * P], ident[:])
                 source = turned[:].rearrange("q (k u) i -> q k i u", u=2)
                 target = grouped_words[:, :, r * P : (r + 1) * P, :]
-                if r % PACK == PACK - 1:
+                if copy_engines[r] == VECTOR:
                     nc.vector.tensor_copy(out=target, in_=source)
                 else:
                     nc.scalar.copy(out=target, in_=source)
             return grouped
 
-        def quantise_rows(grouped, n_tiles, name):
-            codes = keep.tile([P, D_PASSES, n_tiles * P], U32, name=name + "_codes", align_bytes=64)
-            scales = keep.tile([P, D_PASSES, n_tiles * P], U8, name=name + "_scales", align_bytes=64)
+        def quantise_rows(grouped, name):
+            codes = keep.tile([P, D_PASSES, BLOCK], U32, name=name + "_codes", align_bytes=64)
+            scales = keep.tile([P, D_PASSES, BLOCK], U8, name=name + "_scales", align_bytes=64)
             nc.vector.quantize_mx(
                 out=codes[:].rearrange("q k c -> q (k c)").bitcast(FP8X4),
                 scales=scales[:].rearrange("q k c -> q (k c)"),
@@ -117,172 +120,259 @@ def tile_tverskylayer_pa_kernel(tc, x, features, prototypes, alpha, beta, theta,
         silu = {}
         tanh = {}
 
-        def first_contraction(j, g):
-            silu[j, g] = silu_pool.tile([P, PACK, BLOCK], F32, name="silu_v", tag="silu")
-            tanh[j, g] = stage.tile([P, PACK, BLOCK], F32, name="tanh_v", tag="tanh")
+        def first_contraction(j, g, pair):
+            if pair == 0:
+                silu[j, g] = silu_pool.tile([P, PACK, BLOCK], F32, name="silu_v", tag="silu")
+                tanh[j, g] = stage.tile([P, PACK, BLOCK], F32, name="tanh_v", tag="tanh")
             c_codes, c_scales = block_mx[j]
-            f_codes, f_scales = f_mx[g]
-            for pair in range(PACK // 2):
-                v = work.tile([P, 2, BLOCK], F32, tag="work")
-                for s in range(2):
-                    m_cols = slice((2 * pair + s) * P, (2 * pair + s + 1) * P)
-                    for k in range(D_PASSES):
-                        nc.tensor.matmul_mx(
-                            out=v[:, s, :],
-                            lhsT=f_codes[:, k, m_cols].bitcast(FP8X4),
-                            lhsT_scale=f_scales[:, k, m_cols],
-                            rhs=c_codes[:, k, :].bitcast(FP8X4),
-                            rhs_scale=c_scales[:, k, :],
-                            start=(k == 0),
-                            stop=(k == D_PASSES - 1),
-                        )
-                ts = slice(2 * pair, 2 * pair + 2)
-                nc.scalar.activation(out=silu[j, g][:, ts, :], in_=v[:], func=FUNC.Silu)
-                nc.scalar.activation(out=tanh[j, g][:, ts, :], in_=v[:], func=FUNC.Tanh, scale=0.5)
+            f_codes, f_scales = f_mx[g, pair]
+            v = work.tile([P, 2, BLOCK], F32, tag="work")
+            for s in range(2):
+                m_cols = slice(s * P, (s + 1) * P)
+                for k in range(D_PASSES):
+                    nc.tensor.matmul_mx(
+                        out=v[:, s, :],
+                        lhsT=f_codes[:, k, m_cols].bitcast(FP8X4),
+                        lhsT_scale=f_scales[:, k, m_cols],
+                        rhs=c_codes[:, k, :].bitcast(FP8X4),
+                        rhs_scale=c_scales[:, k, :],
+                        start=(k == 0),
+                        stop=(k == D_PASSES - 1),
+                    )
+            ts = slice(2 * pair, 2 * pair + 2)
+            nc.scalar.activation(out=silu[j, g][:, ts, :], in_=v[:], func=FUNC.Silu)
+            nc.scalar.activation(out=tanh[j, g][:, ts, :], in_=v[:], func=FUNC.Tanh, scale=0.5)
 
         second_mx = {}
+        rounded = {}
 
-        def round_and_quantise(j, g):
-            if g == 0:
-                pool = keep if j == 0 else proto_mx
-                codes = pool.tile([P, F_PASSES, 2, BLOCK], U32, name="second_codes", align_bytes=64)
-                scales = pool.tile([P, F_PASSES, 2, BLOCK], U8, name="second_scales", align_bytes=64)
-                second_mx[j] = (codes, scales)
-            codes, scales = second_mx[j]
-            rounded = stage.tile([P, 2, BLOCK, PACK], BF16, align_bytes=64)
+        def round_prod(j, g):
+            rounded[j, g] = stage.tile([P, 2, BLOCK, PACK], BF16, name="rounded_pass", tag="rounded", align_bytes=64)
             nc.vector.tensor_copy(
-                out=rounded[:, PROD, :, :].rearrange("p (c i) t -> p c t i", i=RUN),
+                out=rounded[j, g][:, PROD, :, :].rearrange("p (c i) t -> p c t i", i=RUN),
                 in_=silu[j, g][:].rearrange("p t (c i) -> p c t i", i=RUN),
             )
+
+        def round_sig(j, g):
             nc.vector.tensor_scalar(
-                out=rounded[:, SIG, :, :].rearrange("p (c i) t -> p c t i", i=RUN),
+                out=rounded[j, g][:, SIG, :, :].rearrange("p (c i) t -> p c t i", i=RUN),
                 in0=tanh[j, g][:].rearrange("p t (c i) -> p c t i", i=RUN),
                 scalar1=0.5,
                 scalar2=0.5,
                 op0=ALU.mult,
                 op1=ALU.add,
             )
+
+        def quantise_pass(j, g):
+            if g == 0:
+                pool = keep if j == 0 else proto_mx
+                codes = pool.tile([P, F_PASSES, 2, BLOCK], U32, name="second_codes", align_bytes=64)
+                scales = pool.tile([P, F_PASSES, 2, BLOCK], U8, name="second_scales", align_bytes=64)
+                second_mx[j] = (codes, scales)
+            codes, scales = second_mx[j]
             nc.vector.quantize_mx(
                 out=codes[:, g, :, :].rearrange("p k c -> p (k c)").bitcast(FP8X4),
                 scales=scales[:, g, :, :].rearrange("p k c -> p (k c)"),
-                in_=rounded[:].rearrange("p k c t -> p (k c t)"),
+                in_=rounded[j, g][:].rearrange("p k c t -> p (k c t)"),
             )
 
         sums = {}
-        spread = {}
+        folded = {}
+        total = {}
 
-        def add_up(j):
-            sums[j] = sums_pool.tile([P, 2 * BLOCK_TILES, P], F32, name="sums_bank", tag="sums")
+        def fold(j, g):
+            folded[j, g] = stage.tile([P, PACK // 2, BLOCK], F32, name="folded_pass", tag="folded")
+            nc.vector.tensor_add(out=folded[j, g][:], in0=silu[j, g][:, 0:2, :], in1=silu[j, g][:, 2:4, :])
+
+        def add_up(j, passes, part=0, n_parts=1):
+            if part == 0:
+                sums[j] = sums_pool.tile([P, BLOCK_TILES, n_parts, P], F32, name="sums_bank", tag="sums")
             for ct in range(BLOCK_TILES):
                 cols = slice(ct * P, (ct + 1) * P)
-                for g in range(F_PASSES):
-                    for t in range(PACK):
-                        nc.tensor.matmul(
-                            out=sums[j][:, ct, :],
-                            lhsT=silu[j, g][:, t, cols],
-                            rhs=ident[:],
-                            start=(g == 0 and t == 0),
-                            stop=(g == F_PASSES - 1 and t == PACK - 1),
-                            is_transpose=True,
-                        )
-            total = stage.tile([P, BLOCK_TILES], F32)
-            nc.vector.tensor_reduce(
-                out=total[:], in_=sums[j][:, 0:BLOCK_TILES, :], axis=mybir.AxisListType.X, op=ALU.add
-            )
-            if j == 0:
-                nc.vector.tensor_scalar_mul(
-                    out=x_bias[:], in0=total[:], scalar1=gains[:, NEG_ALPHA : NEG_ALPHA + 1]
-                )
-            else:
-                spread[j] = stage.tile([P, BLOCK_TILES, P], F32, name="spread_sum", tag="spread")
-                for ct in range(BLOCK_TILES):
-                    nc.vector.tensor_scalar(
-                        out=spread[j][:, ct, :],
-                        in0=ones[:],
-                        scalar1=total[:, ct : ct + 1],
-                        scalar2=gains[:, NEG_BETA : NEG_BETA + 1],
-                        op0=ALU.mult,
-                        op1=ALU.mult,
+                terms = []
+                for g in passes:
+                    source = folded.get((j, g), silu[j, g])
+                    terms += [source[:, t, cols] for t in range(source.shape[1])]
+                for i, term in enumerate(terms):
+                    nc.tensor.matmul(
+                        out=sums[j][:, ct, part, :],
+                        lhsT=term,
+                        rhs=ident[:],
+                        start=(i == 0),
+                        stop=(i == len(terms) - 1),
+                        is_transpose=True,
                     )
+
+        def finish_sum(j):
+            total[j] = stage.tile([P, BLOCK_TILES], F32, name="total", tag="total")
+            nc.vector.tensor_reduce(
+                out=total[j][:],
+                in_=sums[j][:].rearrange("p c h f -> p c (h f)"),
+                axis=mybir.AxisListType.X,
+                op=ALU.add,
+            )
 
         result = {}
 
         def start_result(j):
+            spread = sums[j][:].rearrange("p c h f -> p (c h f)")
             for ct in range(BLOCK_TILES):
-                nc.tensor.transpose(sums[j][:, BLOCK_TILES + ct, :], spread[j][:, ct, :], ident[:])
+                nc.tensor.matmul(
+                    out=spread[:, ct * P : (ct + 1) * P],
+                    lhsT=total[j][:, ct : ct + 1].to_broadcast([P, P]),
+                    rhs=ident[:],
+                    start=True,
+                    stop=True,
+                )
             result[j] = stage.tile([P, BLOCK_TILES, BLOCK], F32, name="result", tag="result")
             for bt in range(BLOCK_TILES):
                 nc.scalar.activation(
                     out=result[j][:, bt, :],
-                    in_=sums[j][:, BLOCK_TILES:, :].rearrange("p a c -> p (a c)"),
+                    in_=spread[:, :BLOCK],
                     func=FUNC.Identity,
                     bias=x_bias[:, bt : bt + 1],
-                    scale=1.0,
+                    scale=gains[:, NEG_BETA : NEG_BETA + 1],
                 )
 
         out_view = out.rearrange("(bt p) n -> p bt n", p=P)
 
-        def second_contraction(j):
+        def multiply(j, x_kind, bt, proto_kinds, bank, passes):
             l_codes, l_scales = second_mx[0]
             r_codes, r_scales = second_mx[j]
-            for x_kind, proto_kind, gain in ((PROD, PROD, THETA), (SIG, PROD, BETA), (PROD, SIG, ALPHA)):
-                acc = acc_pool.tile([P, BLOCK_TILES, BLOCK], F32, tag="acc")
-                for bt in range(BLOCK_TILES):
-                    m_cols = slice(bt * P, (bt + 1) * P)
-                    for g in range(F_PASSES):
-                        nc.tensor.matmul_mx(
-                            out=acc[:, bt, :],
-                            lhsT=l_codes[:, g, x_kind, m_cols].bitcast(FP8X4),
-                            lhsT_scale=l_scales[:, g, x_kind, m_cols],
-                            rhs=r_codes[:, g, proto_kind, :].bitcast(FP8X4),
-                            rhs_scale=r_scales[:, g, proto_kind, :],
-                            start=(g == 0),
-                            stop=(g == F_PASSES - 1),
-                        )
-                nc.vector.scalar_tensor_tensor(
-                    out=result[j][:],
-                    in0=acc[:],
-                    scalar=gains[:, gain : gain + 1],
-                    in1=result[j][:],
-                    op0=ALU.mult,
-                    op1=ALU.add,
+            m_cols = slice(bt * P, (bt + 1) * P)
+            for g in passes:
+                nc.tensor.matmul_mx(
+                    out=bank,
+                    lhsT=l_codes[:, g, x_kind, m_cols].bitcast(FP8X4),
+                    lhsT_scale=l_scales[:, g, x_kind, m_cols],
+                    rhs=r_codes[:, g, proto_kinds, :].rearrange("p k c -> p (k c)").bitcast(FP8X4),
+                    rhs_scale=r_scales[:, g, proto_kinds, :].rearrange("p k c -> p (k c)"),
+                    start=(g == 0),
+                    stop=(g == F_PASSES - 1),
                 )
-            nc.sync.dma_start(out=out_view[:, :, (j - 1) * BLOCK : j * BLOCK], in_=result[j][:])
 
-        turned = turn_rows(x_raw, BLOCK_TILES, "grouped_block")
-        block_mx[0] = quantise_rows(turned, BLOCK_TILES, "block0")
-        turned = turn_rows(f_raw[0], PACK, "grouped_f")
-        for g in range(F_PASSES):
-            f_mx[g] = quantise_rows(turned, PACK, "f%d" % g)
-            if g + 1 < F_PASSES:
-                turned = turn_rows(f_raw[g + 1], PACK, "grouped_f")
-            else:
-                turned = turn_rows(block_raw[1], BLOCK_TILES, "grouped_block")
-            first_contraction(0, g)
-            if g > 0:
-                round_and_quantise(0, g - 1)
-        block_mx[1] = quantise_rows(turned, BLOCK_TILES, "block1")
-        spread_gains()
+        BOTH, PROD_ONLY = slice(PROD, SIG + 1), slice(PROD, PROD + 1)
 
-        for j in range(1, N_BLOCKS):
-            first_contraction(j, 0)
-            round_and_quantise(j - 1, 3)
-            first_contraction(j, 1)
-            round_and_quantise(j, 0)
-            add_up(j - 1)
-            if j + 1 < N_BLOCKS:
-                turned = turn_rows(block_raw[j + 1], BLOCK_TILES, "grouped_block")
-                block_mx[j + 1] = quantise_rows(turned, BLOCK_TILES, "block%d" % (j + 1))
-            first_contraction(j, 2)
-            round_and_quantise(j, 1)
-            first_contraction(j, 3)
-            round_and_quantise(j, 2)
-            if j > 1:
-                start_result(j - 1)
-                second_contraction(j - 1)
+        def add_product(j, bts, bank, gain):
+            nc.vector.scalar_tensor_tensor(
+                out=result[j][:, bts, :],
+                in0=bank,
+                scalar=gains[:, gain : gain + 1],
+                in1=result[j][:, bts, :],
+                op0=ALU.mult,
+                op1=ALU.add,
+            )
 
-        last = N_BLOCKS - 1
-        round_and_quantise(last, 3)
-        add_up(last)
-        start_result(last)
-        second_contraction(last)
+        def multiply_ax(j, bt, passes=range(F_PASSES), bank=None):
+            if bank is None:
+                bank = acc_pool.tile([P, 2, BLOCK], F32, name="ax_bank", tag="acc")
+            multiply(j, PROD, bt, BOTH, bank[:].rearrange("p k c -> p (k c)"), passes)
+            return bank
+
+        def add_ax(j, bt, bank):
+            add_product(j, slice(bt, bt + 1), bank[:, PROD : PROD + 1, :], THETA)
+            add_product(j, slice(bt, bt + 1), bank[:, SIG : SIG + 1, :], ALPHA)
+
+        def multiply_sx(j):
+            bank = acc_pool.tile([P, BLOCK_TILES, BLOCK], F32, name="sx_bank", tag="acc")
+            for bt in range(BLOCK_TILES):
+                multiply(j, SIG, bt, PROD_ONLY, bank[:, bt, :], range(F_PASSES))
+            return bank
+
+        def store(j, bts=slice(0, BLOCK_TILES)):
+            nc.sync.dma_start(out=out_view[:, bts, (j - 1) * BLOCK : j * BLOCK], in_=result[j][:, bts, :])
+
+        with tc.manual_schedule():
+            def turn_features(i):
+                return turn_rows(f_raw[units[i]], (SCALAR, VECTOR))
+
+            def quantise_features(i, turned):
+                f_mx[units[i]] = quantise_rows(turned, "f%d_%d" % units[i])
+
+            last = N_BLOCKS - 1
+            FOLDED = (0, 1)
+            banks = {}
+            turned_block = {}
+            turned_f = {}
+
+            def multiply_product(j, product):
+                banks[j, product] = multiply_sx(j) if product == BLOCK_TILES else multiply_ax(j, product)
+
+            def add_product_of(j, product):
+                if product == BLOCK_TILES:
+                    add_product(j, slice(0, BLOCK_TILES), banks[j, product][:], BETA)
+                else:
+                    add_ax(j, product, banks[j, product])
+
+            def round_pass(j, g):
+                round_prod(j, g)
+                round_sig(j, g)
+
+            turned_block[0] = turn_rows(block_raw[0], (SCALAR, VECTOR))
+            turned_f[0] = turn_features(0)
+            block_mx[0] = quantise_rows(turned_block[0], "block0")
+            turned_f[1] = turn_features(1)
+            quantise_features(0, turned_f[0])
+            for j in range(N_BLOCKS):
+                for u, (g, pair) in enumerate(units):
+                    if j == 0 and u + 1 < len(units):
+                        quantise_features(u + 1, turned_f[u + 1])
+                    if j == 0 and u + 2 < len(units):
+                        turned_f[u + 2] = turn_features(u + 2)
+                    product = u - (len(units) - 3)
+                    if j > 1 and product == 1:
+                        start_result(j - 1)
+                    if j > 1 and product >= 0:
+                        multiply_product(j - 1, product)
+                    first_contraction(j, g, pair)
+                    if u == 6 and j < last:
+                        block_mx[j + 1] = quantise_rows(turned_block[j + 1], "block%d" % (j + 1))
+                    if u == 3 and j > 0:
+                        add_up(j - 1, range(F_PASSES))
+                    if pair == 0 and (j > 0 or g > 0):
+                        round_pass(*((j, g - 1) if g > 0 else (j - 1, F_PASSES - 1)))
+                    if j > 1 and product >= 1:
+                        add_product_of(j - 1, product - 1)
+                    if j > 2 and u == 0:
+                        add_product_of(j - 2, BLOCK_TILES)
+                        store(j - 2)
+                    if pair == 0 and j > 0 and g - 1 in FOLDED:
+                        fold(j, g - 1)
+                    if u == 3 and j > 0:
+                        finish_sum(j - 1)
+                    if u == 3 and j == 1:
+                        spread_gains()
+                        nc.vector.tensor_scalar_mul(
+                            out=x_bias[:], in0=total[0][:], scalar1=gains[:, NEG_ALPHA : NEG_ALPHA + 1]
+                        )
+                    if pair == 1 and (j > 0 or g > 0):
+                        quantise_pass(*((j, g - 1) if g > 0 else (j - 1, F_PASSES - 1)))
+                    if u == 3 and j < last:
+                        turned_block[j + 1] = turn_rows(block_raw[j + 1], (SCALAR, SCALAR))
+
+            early, late = range(F_PASSES - 1), range(F_PASSES - 1, F_PASSES)
+            add_up(last, early, 0, 2)
+            round_pass(last, F_PASSES - 1)
+            add_product_of(last - 1, BLOCK_TILES)
+            store(last - 1)
+            quantise_pass(last, F_PASSES - 1)
+            add_up(last, late, 1, 2)
+            finish_sum(last)
+            ax = [multiply_ax(last, bt, early) for bt in range(BLOCK_TILES)]
+            sx = [
+                acc_pool.tile([P, BLOCK], F32, name="sx_bank_0", tag="acc"),
+                work.tile([P, BLOCK], F32, name="sx_bank_1", tag="work"),
+            ]
+            multiply(last, SIG, 0, PROD_ONLY, sx[0][:], early)
+            start_result(last)
+            multiply(last, SIG, 1, PROD_ONLY, sx[1][:], early)
+            for bt in range(BLOCK_TILES):
+                multiply_ax(last, bt, late, ax[bt])
+            for bt in range(BLOCK_TILES):
+                multiply(last, SIG, bt, PROD_ONLY, sx[bt][:], late)
+            for kind, gain in ((PROD, THETA), (SIG, ALPHA)):
+                for bt in range(BLOCK_TILES):
+                    add_product(last, slice(bt, bt + 1), ax[bt][:, kind : kind + 1, :], gain)
+            for bt in range(BLOCK_TILES):
+                add_product(last, slice(bt, bt + 1), sx[bt][:].unsqueeze(1), BETA)
+                store(last, slice(bt, bt + 1))

@@ -21,6 +21,7 @@ WORD_TILES = D // 2 // P
 BLOCK = 256
 BLOCK_TILES = BLOCK // P
 N_BLOCKS = (B + N_PROTO) // BLOCK
+WARM_COLS = 512
 RUN = 4
 SCALAR, VECTOR = 0, 1
 PROD, SIG = 0, 1
@@ -77,6 +78,14 @@ def tile_tverskylayer_pa_kernel(tc, x, features, prototypes, alpha, beta, theta,
         nc.vector.memset(ones[:], 1.0)
         warm = const.tile([P, 1], F32)
         nc.scalar.activation(out=warm[:], in_=ones[:, 0:1], func=FUNC.Silu)
+
+        zeros = const.tile([P, WARM_COLS], BF16)
+        nc.gpsimd.memset(zeros[:], 0.0)
+
+        def keep_warm(n):
+            bank = acc_pool.tile([P, WARM_COLS], F32, name="warm_bank", tag="acc")
+            for i in range(n):
+                nc.tensor.matmul(out=bank[:], lhsT=zeros[:, 0:P], rhs=zeros[:], start=True, stop=True)
 
         gains = const.tile([P, 5], F32)
         x_bias = const.tile([P, BLOCK_TILES], F32)
@@ -308,10 +317,13 @@ def tile_tverskylayer_pa_kernel(tc, x, features, prototypes, alpha, beta, theta,
                 round_prod(j, g)
                 round_sig(j, g)
 
+            keep_warm(5)
             turned_block[0] = turn_rows(block_raw[0], (SCALAR, VECTOR))
             turned_f[0] = turn_features(0)
+            keep_warm(2)
             block_mx[0] = quantise_rows(turned_block[0], "block0")
             turned_f[1] = turn_features(1)
+            keep_warm(2)
             quantise_features(0, turned_f[0])
             for j in range(N_BLOCKS):
                 for u, (g, pair) in enumerate(units):

@@ -41,8 +41,7 @@ def tile_tverskylayer_pa_kernel(tc, x, features, prototypes, alpha, beta, theta,
         tc.tile_pool(name="silu", bufs=10) as silu_pool,
         tc.tile_pool(name="stage", bufs=4) as stage,
         tc.tile_pool(name="proto_mx", bufs=3) as proto_mx,
-        tc.psum_pool(name="work", bufs=4) as work,
-        tc.psum_pool(name="sums", bufs=1) as sums_pool,
+        tc.psum_pool(name="work", bufs=5) as work,
         tc.psum_pool(name="acc", bufs=3) as acc_pool,
     ):
         theta_bf = const.tile([P, 1], BF16)
@@ -195,7 +194,7 @@ def tile_tverskylayer_pa_kernel(tc, x, features, prototypes, alpha, beta, theta,
 
         def add_up(j, passes, part=0, n_parts=1):
             if part == 0:
-                sums[j] = sums_pool.tile([P, BLOCK_TILES, n_parts, P], F32, name="sums_bank", tag="sums")
+                sums[j] = acc_pool.tile([P, BLOCK_TILES, n_parts, P], F32, name="sums_bank", tag="acc")
             for ct in range(BLOCK_TILES):
                 cols = slice(ct * P, (ct + 1) * P)
                 terms = []
@@ -221,18 +220,22 @@ def tile_tverskylayer_pa_kernel(tc, x, features, prototypes, alpha, beta, theta,
                 op=ALU.add,
             )
 
+        repeated = {}
+
+        def repeat_sum(j):
+            repeated[j] = stage.tile([P, BLOCK_TILES, P], F32, name="repeated_sum", tag="repeated")
+            for ct in range(BLOCK_TILES):
+                nc.scalar.activation(
+                    out=repeated[j][:, ct, :], in_=ones[:], func=FUNC.Copy, scale=total[j][:, ct : ct + 1]
+                )
+
         result = {}
 
         def start_result(j):
             spread = sums[j][:].rearrange("p c h f -> p (c h f)")
             for ct in range(BLOCK_TILES):
-                nc.tensor.matmul(
-                    out=spread[:, ct * P : (ct + 1) * P],
-                    lhsT=total[j][:, ct : ct + 1].to_broadcast([P, P]),
-                    rhs=ident[:],
-                    start=True,
-                    stop=True,
-                )
+                cols = slice(ct * P, (ct + 1) * P)
+                nc.tensor.transpose(spread[:, cols], repeated[j][:, ct, :], ident[:])
             result[j] = stage.tile([P, BLOCK_TILES, BLOCK], F32, name="result", tag="result")
             for bt in range(BLOCK_TILES):
                 nc.scalar.activation(
@@ -299,7 +302,7 @@ def tile_tverskylayer_pa_kernel(tc, x, features, prototypes, alpha, beta, theta,
                 f_mx[units[i]] = quantise_rows(turned, "f%d_%d" % units[i])
 
             last = N_BLOCKS - 1
-            FOLDED = (0, 1)
+            FOLDED = (0,)
             banks = {}
             turned_block = {}
             turned_f = {}
@@ -313,10 +316,6 @@ def tile_tverskylayer_pa_kernel(tc, x, features, prototypes, alpha, beta, theta,
                 else:
                     add_ax(j, product, banks[j, product])
 
-            def round_pass(j, g):
-                round_prod(j, g)
-                round_sig(j, g)
-
             keep_warm(5)
             turned_block[0] = turn_rows(block_raw[0], (SCALAR, VECTOR))
             turned_f[0] = turn_features(0)
@@ -325,6 +324,12 @@ def tile_tverskylayer_pa_kernel(tc, x, features, prototypes, alpha, beta, theta,
             turned_f[1] = turn_features(1)
             keep_warm(2)
             quantise_features(0, turned_f[0])
+            order = [(j, g) for j in range(N_BLOCKS) for g in range(F_PASSES)]
+
+            def passes_before(j, g, n):
+                i = order.index((j, g)) - n
+                return order[i : i + 1] if i >= 0 else []
+
             for j in range(N_BLOCKS):
                 for u, (g, pair) in enumerate(units):
                     if j == 0 and u + 1 < len(units):
@@ -332,24 +337,28 @@ def tile_tverskylayer_pa_kernel(tc, x, features, prototypes, alpha, beta, theta,
                     if j == 0 and u + 2 < len(units):
                         turned_f[u + 2] = turn_features(u + 2)
                     product = u - (len(units) - 3)
+                    if u == 4 and j > 1:
+                        repeat_sum(j - 1)
                     if j > 1 and product == 1:
                         start_result(j - 1)
-                    if j > 1 and product >= 0:
-                        multiply_product(j - 1, product)
                     first_contraction(j, g, pair)
-                    if u == 6 and j < last:
-                        block_mx[j + 1] = quantise_rows(turned_block[j + 1], "block%d" % (j + 1))
                     if u == 3 and j > 0:
                         add_up(j - 1, range(F_PASSES))
-                    if pair == 0 and (j > 0 or g > 0):
-                        round_pass(*((j, g - 1) if g > 0 else (j - 1, F_PASSES - 1)))
-                    if j > 1 and product >= 1:
-                        add_product_of(j - 1, product - 1)
-                    if j > 2 and u == 0:
-                        add_product_of(j - 2, BLOCK_TILES)
-                        store(j - 2)
-                    if pair == 0 and j > 0 and g - 1 in FOLDED:
-                        fold(j, g - 1)
+                    if u == 6 and j < last:
+                        block_mx[j + 1] = quantise_rows(turned_block[j + 1], "block%d" % (j + 1))
+                    if pair == 0:
+                        for jj, gg in passes_before(j, g, 1):
+                            if jj > 0 and gg in FOLDED:
+                                fold(jj, gg)
+                        for jj, gg in passes_before(j, g, 2):
+                            quantise_pass(jj, gg)
+                        for jj, gg in passes_before(j, g, 1):
+                            round_prod(jj, gg)
+                    else:
+                        for jj, gg in passes_before(j, g, 1):
+                            round_sig(jj, gg)
+                    if j > 1 and product >= 0:
+                        multiply_product(j - 1, product)
                     if u == 3 and j > 0:
                         finish_sum(j - 1)
                     if u == 3 and j == 1:
@@ -357,22 +366,28 @@ def tile_tverskylayer_pa_kernel(tc, x, features, prototypes, alpha, beta, theta,
                         nc.vector.tensor_scalar_mul(
                             out=x_bias[:], in0=total[0][:], scalar1=gains[:, NEG_ALPHA : NEG_ALPHA + 1]
                         )
-                    if pair == 1 and (j > 0 or g > 0):
-                        quantise_pass(*((j, g - 1) if g > 0 else (j - 1, F_PASSES - 1)))
+                    if j > 1 and product >= 1:
+                        add_product_of(j - 1, product - 1)
+                    if j > 2 and u == 0:
+                        add_product_of(j - 2, BLOCK_TILES)
+                        store(j - 2)
                     if u == 3 and j < last:
                         turned_block[j + 1] = turn_rows(block_raw[j + 1], (SCALAR, SCALAR))
 
             early, late = range(F_PASSES - 1), range(F_PASSES - 1, F_PASSES)
             add_up(last, early, 0, 2)
-            round_pass(last, F_PASSES - 1)
+            quantise_pass(last, F_PASSES - 2)
+            round_prod(last, F_PASSES - 1)
             add_product_of(last - 1, BLOCK_TILES)
             store(last - 1)
-            quantise_pass(last, F_PASSES - 1)
+            round_sig(last, F_PASSES - 1)
             add_up(last, late, 1, 2)
             finish_sum(last)
+            repeat_sum(last)
+            quantise_pass(last, F_PASSES - 1)
             ax = [multiply_ax(last, bt, early) for bt in range(BLOCK_TILES)]
             sx = [
-                acc_pool.tile([P, BLOCK], F32, name="sx_bank_0", tag="acc"),
+                work.tile([P, BLOCK], F32, name="sx_bank_0", tag="work"),
                 work.tile([P, BLOCK], F32, name="sx_bank_1", tag="work"),
             ]
             multiply(last, SIG, 0, PROD_ONLY, sx[0][:], early)

@@ -40,6 +40,7 @@ def tile_tverskylayer_pa_kernel(tc, x, features, prototypes, alpha, beta, theta,
         tc.tile_pool(name="grouped", bufs=4) as grouped_pool,
         tc.tile_pool(name="silu", bufs=10) as silu_pool,
         tc.tile_pool(name="stage", bufs=4) as stage,
+        tc.tile_pool(name="once", bufs=1) as once,
         tc.tile_pool(name="proto_mx", bufs=3) as proto_mx,
         tc.psum_pool(name="work", bufs=5) as work,
         tc.psum_pool(name="acc", bufs=3) as acc_pool,
@@ -131,7 +132,7 @@ def tile_tverskylayer_pa_kernel(tc, x, features, prototypes, alpha, beta, theta,
         def first_contraction(j, g, pair):
             if pair == 0:
                 silu[j, g] = silu_pool.tile([P, PACK, BLOCK], F32, name="silu_v", tag="silu")
-                tanh[j, g] = stage.tile([P, PACK, BLOCK], F32, name="tanh_v", tag="tanh")
+                tanh[j, g] = stage.tile([P, PACK // 2, BLOCK, 2], F32, name="tanh_v", tag="tanh")
             c_codes, c_scales = block_mx[j]
             f_codes, f_scales = f_mx[g, pair]
             v = work.tile([P, 2, BLOCK], F32, tag="work")
@@ -149,7 +150,9 @@ def tile_tverskylayer_pa_kernel(tc, x, features, prototypes, alpha, beta, theta,
                     )
             ts = slice(2 * pair, 2 * pair + 2)
             nc.scalar.activation(out=silu[j, g][:, ts, :], in_=v[:], func=FUNC.Silu)
-            nc.scalar.activation(out=tanh[j, g][:, ts, :], in_=v[:], func=FUNC.Tanh, scale=0.5)
+            nc.scalar.activation(
+                out=tanh[j, g][:, pair, :, :], in_=v[:].rearrange("p s c -> p c s"), func=FUNC.Tanh, scale=0.5
+            )
 
         second_mx = {}
         rounded = {}
@@ -163,8 +166,8 @@ def tile_tverskylayer_pa_kernel(tc, x, features, prototypes, alpha, beta, theta,
 
         def round_sig(j, g):
             nc.vector.tensor_scalar(
-                out=rounded[j, g][:, SIG, :, :].rearrange("p (c i) t -> p c t i", i=RUN),
-                in0=tanh[j, g][:].rearrange("p t (c i) -> p c t i", i=RUN),
+                out=rounded[j, g][:, SIG, :, :].rearrange("p c (a s) -> p c a s", s=2),
+                in0=tanh[j, g][:].rearrange("p a c s -> p c a s"),
                 scalar1=0.5,
                 scalar2=0.5,
                 op0=ALU.mult,
@@ -219,6 +222,17 @@ def tile_tverskylayer_pa_kernel(tc, x, features, prototypes, alpha, beta, theta,
                 axis=mybir.AxisListType.X,
                 op=ALU.add,
             )
+
+        def finish_sum_on_scalar(j):
+            total[j] = stage.tile([P, BLOCK_TILES], F32, name="total", tag="total")
+            copied = once.tile([P, BLOCK_TILES, BLOCK], F32, name="copied_sums")
+            for ct in range(BLOCK_TILES):
+                nc.scalar.activation(
+                    out=copied[:, ct, :],
+                    in_=sums[j][:, ct, :, :].rearrange("p h f -> p (h f)"),
+                    func=FUNC.Identity,
+                    accum_out=total[j][:, ct : ct + 1],
+                )
 
         repeated = {}
 
@@ -302,6 +316,7 @@ def tile_tverskylayer_pa_kernel(tc, x, features, prototypes, alpha, beta, theta,
                 f_mx[units[i]] = quantise_rows(turned, "f%d_%d" % units[i])
 
             last = N_BLOCKS - 1
+            FOLDED_LAST = (0, 1, 2)
             FOLDED = (0,)
             banks = {}
             turned_block = {}
@@ -348,7 +363,7 @@ def tile_tverskylayer_pa_kernel(tc, x, features, prototypes, alpha, beta, theta,
                         block_mx[j + 1] = quantise_rows(turned_block[j + 1], "block%d" % (j + 1))
                     if pair == 0:
                         for jj, gg in passes_before(j, g, 1):
-                            if jj > 0 and gg in FOLDED:
+                            if jj > 0 and gg in (FOLDED_LAST if jj == last else FOLDED):
                                 fold(jj, gg)
                         for jj, gg in passes_before(j, g, 2):
                             quantise_pass(jj, gg)
@@ -378,14 +393,17 @@ def tile_tverskylayer_pa_kernel(tc, x, features, prototypes, alpha, beta, theta,
             add_up(last, early, 0, 2)
             quantise_pass(last, F_PASSES - 2)
             round_prod(last, F_PASSES - 1)
-            add_product_of(last - 1, BLOCK_TILES)
-            store(last - 1)
             round_sig(last, F_PASSES - 1)
             add_up(last, late, 1, 2)
-            finish_sum(last)
+            finish_sum_on_scalar(last)
             repeat_sum(last)
             quantise_pass(last, F_PASSES - 1)
-            ax = [multiply_ax(last, bt, early) for bt in range(BLOCK_TILES)]
+            add_product_of(last - 1, BLOCK_TILES)
+            store(last - 1)
+            ax = [
+                multiply_ax(last, 0, early),
+                multiply_ax(last, 1, early, work.tile([P, 2, BLOCK], F32, name="ax_bank_1", tag="work")),
+            ]
             sx = [
                 work.tile([P, BLOCK], F32, name="sx_bank_0", tag="work"),
                 work.tile([P, BLOCK], F32, name="sx_bank_1", tag="work"),

@@ -22,6 +22,8 @@ BLOCK = 256
 BLOCK_TILES = BLOCK // P
 N_BLOCKS = (B + N_PROTO) // BLOCK
 WARM_COLS = 512
+SQUARE = 32
+FIRST_SQUARES = 3
 RUN = 4
 SCALAR, VECTOR = 0, 1
 PROD, SIG = 0, 1
@@ -66,8 +68,21 @@ def tile_tverskylayer_pa_kernel(tc, x, features, prototypes, alpha, beta, theta,
             if i == 6:
                 block_raw[1] = load_rows("p_raw1", p_source[0])
             f_raw[g, pair] = load_rows("f_raw%d_%d" % (g, pair), f_source[g, pair], tile_by_tile=(i == 0))
+        squares = prototypes.rearrange(
+            "(j n r) (k u h i) -> j h u k r n i", r=SQUARE // 2, n=SQUARE // 2, k=D_PASSES, u=2, h=P // SQUARE
+        )
         for j in range(2, N_BLOCKS):
-            block_raw[j] = load_rows("p_raw%d" % j, p_source[j - 1])
+            if j < FIRST_SQUARES:
+                block_raw[j] = load_rows("p_raw%d" % j, p_source[j - 1])
+                continue
+            block_raw[j] = raw.tile([P, D_PASSES, SQUARE // 2, 2 * SQUARE], BF16, name="p_raw%d" % j, align_bytes=64)
+            for k in range(D_PASSES):
+                for h in range(P // SQUARE):
+                    for u in range(2):
+                        nc.sync.dma_start(
+                            out=block_raw[j][h * SQUARE + u : (h + 1) * SQUARE : 2, k, :, :],
+                            in_=squares[j - 1, h, u, k],
+                        )
         nc.sync.dma_start(out=theta_bf[:], in_=theta.partition_broadcast(P))
         nc.sync.dma_start(out=alpha_bf[:], in_=alpha.partition_broadcast(P))
         nc.sync.dma_start(out=beta_bf[:], in_=beta.partition_broadcast(P))
@@ -112,6 +127,15 @@ def tile_tverskylayer_pa_kernel(tc, x, features, prototypes, alpha, beta, theta,
                     nc.vector.tensor_copy(out=target, in_=source)
                 else:
                     nc.scalar.copy(out=target, in_=source)
+            return grouped
+
+        def turn_squares(rows):
+            grouped = grouped_pool.tile([P, D_PASSES, BLOCK, PACK], BF16, align_bytes=64)
+            for k in range(D_PASSES):
+                nc.vector.transpose(
+                    out=grouped[:, k, :, :].rearrange("q c f -> q (c f)").bitcast(F32),
+                    in_=rows[:, k, :, :].rearrange("p n i -> p (n i)").bitcast(F32),
+                )
             return grouped
 
         def quantise_rows(grouped, name):
@@ -316,8 +340,7 @@ def tile_tverskylayer_pa_kernel(tc, x, features, prototypes, alpha, beta, theta,
                 f_mx[units[i]] = quantise_rows(turned, "f%d_%d" % units[i])
 
             last = N_BLOCKS - 1
-            FOLDED_LAST = (0, 1, 2)
-            FOLDED = (0,)
+            FOLDED = (0, 1, 2)
             banks = {}
             turned_block = {}
             turned_f = {}
@@ -363,7 +386,7 @@ def tile_tverskylayer_pa_kernel(tc, x, features, prototypes, alpha, beta, theta,
                         block_mx[j + 1] = quantise_rows(turned_block[j + 1], "block%d" % (j + 1))
                     if pair == 0:
                         for jj, gg in passes_before(j, g, 1):
-                            if jj > 0 and gg in (FOLDED_LAST if jj == last else FOLDED):
+                            if jj == last and gg in FOLDED:
                                 fold(jj, gg)
                         for jj, gg in passes_before(j, g, 2):
                             quantise_pass(jj, gg)
@@ -387,7 +410,10 @@ def tile_tverskylayer_pa_kernel(tc, x, features, prototypes, alpha, beta, theta,
                         add_product_of(j - 2, BLOCK_TILES)
                         store(j - 2)
                     if u == 3 and j < last:
-                        turned_block[j + 1] = turn_rows(block_raw[j + 1], (SCALAR, SCALAR))
+                        if j + 1 < FIRST_SQUARES:
+                            turned_block[j + 1] = turn_rows(block_raw[j + 1], (SCALAR, SCALAR))
+                        else:
+                            turned_block[j + 1] = turn_squares(block_raw[j + 1])
 
             early, late = range(F_PASSES - 1), range(F_PASSES - 1, F_PASSES)
             add_up(last, early, 0, 2)

import concourse.mybir as mybir
from concourse.masks import make_identity

F32 = mybir.dt.float32
BF16 = mybir.dt.bfloat16
U32 = mybir.dt.uint32
U8 = mybir.dt.uint8
FP8X4 = mybir.dt.float8_e4m3fn_x4
FUNC = mybir.ActivationFunctionType
ALU = mybir.AluOpType

P = 128
PACK = 4
K_PASS = P * PACK

B, D, F, N_PROTO = 256, 1024, 2048, 1024
D_PASSES = D // K_PASS
F_PASSES = F // K_PASS
WORD_TILES = D // 2 // P

BLOCK = 256
BLOCK_TILES = BLOCK // P
N_BLOCKS = (B + N_PROTO) // BLOCK
WARM_COLS = 512
SQUARE = 32
FIRST_SQUARES = 3
RUN = 4
SCALAR, VECTOR = 0, 1
PROD, SIG = 0, 1

THETA, ALPHA, BETA, NEG_ALPHA, NEG_BETA = 0, 1, 2, 3, 4

FLOPS = 2 * (B + N_PROTO) * F * D + 3 * 2 * B * N_PROTO * F


def tile_tverskylayer_pa_kernel(tc, x, features, prototypes, alpha, beta, theta, out):
    nc = tc.nc
    with (
        tc.tile_pool(name="const", bufs=1) as const,
        tc.tile_pool(name="raw", bufs=1) as raw,
        tc.tile_pool(name="keep", bufs=1) as keep,
        tc.tile_pool(name="grouped", bufs=4) as grouped_pool,
        tc.tile_pool(name="silu", bufs=10) as silu_pool,
        tc.tile_pool(name="stage", bufs=4) as stage,
        tc.tile_pool(name="once", bufs=1) as once,
        tc.tile_pool(name="proto_mx", bufs=3) as proto_mx,
        tc.psum_pool(name="work", bufs=5) as work,
        tc.psum_pool(name="acc", bufs=3) as acc_pool,
    ):
        theta_bf = const.tile([P, 1], BF16)
        alpha_bf = const.tile([P, 1], BF16)
        beta_bf = const.tile([P, 1], BF16)
        def load_rows(name, source, tile_by_tile=False):
            rows = raw.tile([P, BLOCK_TILES, D], BF16, name=name)
            if tile_by_tile:
                for r in range(BLOCK_TILES):
                    nc.sync.dma_start(out=rows[:, r, :], in_=source[:, r, :])
            else:
                nc.sync.dma_start(out=rows[:], in_=source)
            return rows

        f_source = features.rearrange("(g p pair s) d -> g pair p s d", g=F_PASSES, p=P, pair=2)
        p_source = prototypes.rearrange("(j r p) d -> j p r d", r=BLOCK_TILES, p=P)
        units = [(g, pair) for g in range(F_PASSES) for pair in range(2)]
        block_raw = {0: load_rows("x_raw", x.rearrange("(r p) d -> p r d", p=P), tile_by_tile=True)}
        f_raw = {}
        for i, (g, pair) in enumerate(units):
            if i == 6:
                block_raw[1] = load_rows("p_raw1", p_source[0])
            f_raw[g, pair] = load_rows("f_raw%d_%d" % (g, pair), f_source[g, pair], tile_by_tile=(i == 0))
        squares = prototypes.rearrange(
            "(j n r) (k u h i) -> j h u k r n i", r=SQUARE // 2, n=SQUARE // 2, k=D_PASSES, u=2, h=P // SQUARE
        )
        for j in range(2, N_BLOCKS):
            if j < FIRST_SQUARES:
                block_raw[j] = load_rows("p_raw%d" % j, p_source[j - 1])
                continue
            block_raw[j] = raw.tile([P, D_PASSES, SQUARE // 2, 2 * SQUARE], BF16, name="p_raw%d" % j, align_bytes=64)
            for k in range(D_PASSES):
                for h in range(P // SQUARE):
                    for u in range(2):
                        nc.sync.dma_start(
                            out=block_raw[j][h * SQUARE + u : (h + 1) * SQUARE : 2, k, :, :],
                            in_=squares[j - 1, h, u, k],
                        )
        nc.sync.dma_start(out=theta_bf[:], in_=theta.partition_broadcast(P))
        nc.sync.dma_start(out=alpha_bf[:], in_=alpha.partition_broadcast(P))
        nc.sync.dma_start(out=beta_bf[:], in_=beta.partition_broadcast(P))

        ident = const.tile([P, P], F32)
        make_identity(nc, ident[:])
        ones = const.tile([P, P], F32)
        nc.vector.memset(ones[:], 1.0)
        warm = const.tile([P, 1], F32)
        nc.scalar.activation(out=warm[:], in_=ones[:, 0:1], func=FUNC.Silu)

        zeros = const.tile([P, WARM_COLS], BF16)
        nc.gpsimd.memset(zeros[:], 0.0)

        def keep_warm(n):
            bank = acc_pool.tile([P, WARM_COLS], F32, name="warm_bank", tag="acc")
            for i in range(n):
                nc.tensor.matmul(out=bank[:], lhsT=zeros[:, 0:P], rhs=zeros[:], start=True, stop=True)

        gains = const.tile([P, 5], F32)
        x_bias = const.tile([P, BLOCK_TILES], F32)

        def spread_gains():
            nc.vector.tensor_copy(out=gains[:, THETA : THETA + 1], in_=theta_bf[:])
            nc.vector.tensor_copy(out=gains[:, ALPHA : ALPHA + 1], in_=alpha_bf[:])
            nc.vector.tensor_copy(out=gains[:, BETA : BETA + 1], in_=beta_bf[:])
            nc.vector.tensor_scalar_mul(
                out=gains[:, NEG_ALPHA : NEG_BETA + 1], in0=gains[:, ALPHA : BETA + 1], scalar1=-1.0
            )

        def turn_rows(rows, copy_engines):
            grouped = grouped_pool.tile([P, D_PASSES, BLOCK, PACK], BF16, align_bytes=64)
            row_words = rows[:].bitcast(F32)
            grouped_words = grouped[:].bitcast(F32)
            for r in range(BLOCK_TILES):
                turned = work.tile([P, WORD_TILES, P], F32, tag="work")
                for w in range(WORD_TILES):
                    nc.tensor.transpose(turned[:, w, :], row_words[:, r, w * P : (w + 1) * P], ident[:])
                source = turned[:].rearrange("q (k u) i -> q k i u", u=2)
                target = grouped_words[:, :, r * P : (r + 1) * P, :]
                if copy_engines[r] == VECTOR:
                    nc.vector.tensor_copy(out=target, in_=source)
                else:
                    nc.scalar.copy(out=target, in_=source)
            return grouped

        def turn_squares(rows):
            grouped = grouped_pool.tile([P, D_PASSES, BLOCK, PACK], BF16, align_bytes=64)
            for k in range(D_PASSES):
                nc.vector.transpose(
                    out=grouped[:, k, :, :].rearrange("q c f -> q (c f)").bitcast(F32),
                    in_=rows[:, k, :, :].rearrange("p n i -> p (n i)").bitcast(F32),
                )
            return grouped

        def quantise_rows(grouped, name):
            codes = keep.tile([P, D_PASSES, BLOCK], U32, name=name + "_codes", align_bytes=64)
            scales = keep.tile([P, D_PASSES, BLOCK], U8, name=name + "_scales", align_bytes=64)
            nc.vector.quantize_mx(
                out=codes[:].rearrange("q k c -> q (k c)").bitcast(FP8X4),
                scales=scales[:].rearrange("q k c -> q (k c)"),
                in_=grouped[:].rearrange("q k c f -> q (k c f)"),
            )
            return codes, scales

        f_mx = {}
        block_mx = {}
        silu = {}
        tanh = {}

        def first_contraction(j, g, pair):
            if pair == 0:
                silu[j, g] = silu_pool.tile([P, PACK, BLOCK], F32, name="silu_v", tag="silu")
                tanh[j, g] = stage.tile([P, PACK // 2, BLOCK, 2], F32, name="tanh_v", tag="tanh")
            c_codes, c_scales = block_mx[j]
            f_codes, f_scales = f_mx[g, pair]
            v = work.tile([P, 2, BLOCK], F32, tag="work")
            for s in range(2):
                m_cols = slice(s * P, (s + 1) * P)
                for k in range(D_PASSES):
                    nc.tensor.matmul_mx(
                        out=v[:, s, :],
                        lhsT=f_codes[:, k, m_cols].bitcast(FP8X4),
                        lhsT_scale=f_scales[:, k, m_cols],
                        rhs=c_codes[:, k, :].bitcast(FP8X4),
                        rhs_scale=c_scales[:, k, :],
                        start=(k == 0),
                        stop=(k == D_PASSES - 1),
                    )
            ts = slice(2 * pair, 2 * pair + 2)
            nc.scalar.activation(out=silu[j, g][:, ts, :], in_=v[:], func=FUNC.Silu)
            nc.scalar.activation(
                out=tanh[j, g][:, pair, :, :], in_=v[:].rearrange("p s c -> p c s"), func=FUNC.Tanh, scale=0.5
            )

        second_mx = {}
        rounded = {}

        def round_prod(j, g):
            rounded[j, g] = stage.tile([P, 2, BLOCK, PACK], BF16, name="rounded_pass", tag="rounded", align_bytes=64)
            nc.vector.tensor_copy(
                out=rounded[j, g][:, PROD, :, :].rearrange("p (c i) t -> p c t i", i=RUN),
                in_=silu[j, g][:].rearrange("p t (c i) -> p c t i", i=RUN),
            )

        def round_sig(j, g):
            nc.vector.tensor_scalar(
                out=rounded[j, g][:, SIG, :, :].rearrange("p c (a s) -> p c a s", s=2),
                in0=tanh[j, g][:].rearrange("p a c s -> p c a s"),
                scalar1=0.5,
                scalar2=0.5,
                op0=ALU.mult,
                op1=ALU.add,
            )

        def quantise_pass(j, g):
            if g == 0:
                pool = keep if j == 0 else proto_mx
                codes = pool.tile([P, F_PASSES, 2, BLOCK], U32, name="second_codes", align_bytes=64)
                scales = pool.tile([P, F_PASSES, 2, BLOCK], U8, name="second_scales", align_bytes=64)
                second_mx[j] = (codes, scales)
            codes, scales = second_mx[j]
            nc.vector.quantize_mx(
                out=codes[:, g, :, :].rearrange("p k c -> p (k c)").bitcast(FP8X4),
                scales=scales[:, g, :, :].rearrange("p k c -> p (k c)"),
                in_=rounded[j, g][:].rearrange("p k c t -> p (k c t)"),
            )

        sums = {}
        folded = {}
        total = {}

        def fold(j, g):
            folded[j, g] = stage.tile([P, PACK // 2, BLOCK], F32, name="folded_pass", tag="folded")
            nc.vector.tensor_add(out=folded[j, g][:], in0=silu[j, g][:, 0:2, :], in1=silu[j, g][:, 2:4, :])

        def add_up(j, passes, part=0, n_parts=1):
            if part == 0:
                sums[j] = acc_pool.tile([P, BLOCK_TILES, n_parts, P], F32, name="sums_bank", tag="acc")
            for ct in range(BLOCK_TILES):
                cols = slice(ct * P, (ct + 1) * P)
                terms = []
                for g in passes:
                    source = folded.get((j, g), silu[j, g])
                    terms += [source[:, t, cols] for t in range(source.shape[1])]
                for i, term in enumerate(terms):
                    nc.tensor.matmul(
                        out=sums[j][:, ct, part, :],
                        lhsT=term,
                        rhs=ident[:],
                        start=(i == 0),
                        stop=(i == len(terms) - 1),
                        is_transpose=True,
                    )

        def finish_sum(j):
            total[j] = stage.tile([P, BLOCK_TILES], F32, name="total", tag="total")
            nc.vector.tensor_reduce(
                out=total[j][:],
                in_=sums[j][:].rearrange("p c h f -> p c (h f)"),
                axis=mybir.AxisListType.X,
                op=ALU.add,
            )

        def finish_sum_on_scalar(j):
            total[j] = stage.tile([P, BLOCK_TILES], F32, name="total", tag="total")
            copied = once.tile([P, BLOCK_TILES, BLOCK], F32, name="copied_sums")
            for ct in range(BLOCK_TILES):
                nc.scalar.activation(
                    out=copied[:, ct, :],
                    in_=sums[j][:, ct, :, :].rearrange("p h f -> p (h f)"),
                    func=FUNC.Identity,
                    accum_out=total[j][:, ct : ct + 1],
                )

        repeated = {}

        def repeat_sum(j):
            repeated[j] = stage.tile([P, BLOCK_TILES, P], F32, name="repeated_sum", tag="repeated")
            for ct in range(BLOCK_TILES):
                nc.scalar.activation(
                    out=repeated[j][:, ct, :], in_=ones[:], func=FUNC.Copy, scale=total[j][:, ct : ct + 1]
                )

        result = {}

        def start_result(j):
            spread = sums[j][:].rearrange("p c h f -> p (c h f)")
            for ct in range(BLOCK_TILES):
                cols = slice(ct * P, (ct + 1) * P)
                nc.tensor.transpose(spread[:, cols], repeated[j][:, ct, :], ident[:])
            result[j] = stage.tile([P, BLOCK_TILES, BLOCK], F32, name="result", tag="result")
            for bt in range(BLOCK_TILES):
                nc.scalar.activation(
                    out=result[j][:, bt, :],
                    in_=spread[:, :BLOCK],
                    func=FUNC.Identity,
                    bias=x_bias[:, bt : bt + 1],
                    scale=gains[:, NEG_BETA : NEG_BETA + 1],
                )

        out_view = out.rearrange("(bt p) n -> p bt n", p=P)

        def multiply(j, x_kind, bt, proto_kinds, bank, passes):
            l_codes, l_scales = second_mx[0]
            r_codes, r_scales = second_mx[j]
            m_cols = slice(bt * P, (bt + 1) * P)
            for g in passes:
                nc.tensor.matmul_mx(
                    out=bank,
                    lhsT=l_codes[:, g, x_kind, m_cols].bitcast(FP8X4),
                    lhsT_scale=l_scales[:, g, x_kind, m_cols],
                    rhs=r_codes[:, g, proto_kinds, :].rearrange("p k c -> p (k c)").bitcast(FP8X4),
                    rhs_scale=r_scales[:, g, proto_kinds, :].rearrange("p k c -> p (k c)"),
                    start=(g == 0),
                    stop=(g == F_PASSES - 1),
                )

        BOTH, PROD_ONLY = slice(PROD, SIG + 1), slice(PROD, PROD + 1)

        def add_product(j, bts, bank, gain):
            nc.vector.scalar_tensor_tensor(
                out=result[j][:, bts, :],
                in0=bank,
                scalar=gains[:, gain : gain + 1],
                in1=result[j][:, bts, :],
                op0=ALU.mult,
                op1=ALU.add,
            )

        def multiply_ax(j, bt, passes=range(F_PASSES), bank=None):
            if bank is None:
                bank = acc_pool.tile([P, 2, BLOCK], F32, name="ax_bank", tag="acc")
            multiply(j, PROD, bt, BOTH, bank[:].rearrange("p k c -> p (k c)"), passes)
            return bank

        def add_ax(j, bt, bank):
            add_product(j, slice(bt, bt + 1), bank[:, PROD : PROD + 1, :], THETA)
            add_product(j, slice(bt, bt + 1), bank[:, SIG : SIG + 1, :], ALPHA)

        def multiply_sx(j):
            bank = acc_pool.tile([P, BLOCK_TILES, BLOCK], F32, name="sx_bank", tag="acc")
            for bt in range(BLOCK_TILES):
                multiply(j, SIG, bt, PROD_ONLY, bank[:, bt, :], range(F_PASSES))
            return bank

        def store(j, bts=slice(0, BLOCK_TILES)):
            nc.sync.dma_start(out=out_view[:, bts, (j - 1) * BLOCK : j * BLOCK], in_=result[j][:, bts, :])

        with tc.manual_schedule():
            def turn_features(i):
                return turn_rows(f_raw[units[i]], (SCALAR, VECTOR))

            def quantise_features(i, turned):
                f_mx[units[i]] = quantise_rows(turned, "f%d_%d" % units[i])

            last = N_BLOCKS - 1
            FOLDED = (0, 1, 2)
            banks = {}
            turned_block = {}
            turned_f = {}

            def multiply_product(j, product):
                banks[j, product] = multiply_sx(j) if product == BLOCK_TILES else multiply_ax(j, product)

            def add_product_of(j, product):
                if product == BLOCK_TILES:
                    add_product(j, slice(0, BLOCK_TILES), banks[j, product][:], BETA)
                else:
                    add_ax(j, product, banks[j, product])

            keep_warm(5)
            turned_block[0] = turn_rows(block_raw[0], (SCALAR, VECTOR))
            turned_f[0] = turn_features(0)
            keep_warm(2)
            block_mx[0] = quantise_rows(turned_block[0], "block0")
            turned_f[1] = turn_features(1)
            keep_warm(2)
            quantise_features(0, turned_f[0])
            order = [(j, g) for j in range(N_BLOCKS) for g in range(F_PASSES)]

            def passes_before(j, g, n):
                i = order.index((j, g)) - n
                return order[i : i + 1] if i >= 0 else []

            for j in range(N_BLOCKS):
                for u, (g, pair) in enumerate(units):
                    if j == 0 and u + 1 < len(units):
                        quantise_features(u + 1, turned_f[u + 1])
                    if j == 0 and u + 2 < len(units):
                        turned_f[u + 2] = turn_features(u + 2)
                    product = u - (len(units) - 3)
                    if u == 4 and j > 1:
                        repeat_sum(j - 1)
                    if j > 1 and product == 1:
                        start_result(j - 1)
                    first_contraction(j, g, pair)
                    if u == 3 and j > 0:
                        add_up(j - 1, range(F_PASSES))
                    if u == 6 and j < last:
                        block_mx[j + 1] = quantise_rows(turned_block[j + 1], "block%d" % (j + 1))
                    if pair == 0:
                        for jj, gg in passes_before(j, g, 1):
                            if jj == last and gg in FOLDED:
                                fold(jj, gg)
                        for jj, gg in passes_before(j, g, 2):
                            quantise_pass(jj, gg)
                        for jj, gg in passes_before(j, g, 1):
                            round_prod(jj, gg)
                    else:
                        for jj, gg in passes_before(j, g, 1):
                            round_sig(jj, gg)
                    if j > 1 and product >= 0:
                        multiply_product(j - 1, product)
                    if u == 3 and j > 0:
                        finish_sum(j - 1)
                    if u == 3 and j == 1:
                        spread_gains()
                        nc.vector.tensor_scalar_mul(
                            out=x_bias[:], in0=total[0][:], scalar1=gains[:, NEG_ALPHA : NEG_ALPHA + 1]
                        )
                    if j > 1 and product >= 1:
                        add_product_of(j - 1, product - 1)
                    if j > 2 and u == 0:
                        add_product_of(j - 2, BLOCK_TILES)
                        store(j - 2)
                    if u == 3 and j < last:
                        if j + 1 < FIRST_SQUARES:
                            turned_block[j + 1] = turn_rows(block_raw[j + 1], (SCALAR, SCALAR))
                        else:
                            turned_block[j + 1] = turn_squares(block_raw[j + 1])

            early, late = range(F_PASSES - 1), range(F_PASSES - 1, F_PASSES)
            add_up(last, early, 0, 2)
            quantise_pass(last, F_PASSES - 2)
            round_prod(last, F_PASSES - 1)
            round_sig(last, F_PASSES - 1)
            add_up(last, late, 1, 2)
            finish_sum_on_scalar(last)
            repeat_sum(last)
            quantise_pass(last, F_PASSES - 1)
            add_product_of(last - 1, BLOCK_TILES)
            store(last - 1)
            ax = [
                multiply_ax(last, 0, early),
                multiply_ax(last, 1, early, work.tile([P, 2, BLOCK], F32, name="ax_bank_1", tag="work")),
            ]
            sx = [
                work.tile([P, BLOCK], F32, name="sx_bank_0", tag="work"),
                work.tile([P, BLOCK], F32, name="sx_bank_1", tag="work"),
            ]
            multiply(last, SIG, 0, PROD_ONLY, sx[0][:], early)
            start_result(last)
            multiply(last, SIG, 1, PROD_ONLY, sx[1][:], early)
            for bt in range(BLOCK_TILES):
                multiply_ax(last, bt, late, ax[bt])
            for bt in range(BLOCK_TILES):
                multiply(last, SIG, bt, PROD_ONLY, sx[bt][:], late)
            for kind, gain in ((PROD, THETA), (SIG, ALPHA)):
                for bt in range(BLOCK_TILES):
                    add_product(last, slice(bt, bt + 1), ax[bt][:, kind : kind + 1, :], gain)
            for bt in range(BLOCK_TILES):
                add_product(last, slice(bt, bt + 1), sx[bt][:].unsqueeze(1), BETA)
                store(last, slice(bt, bt + 1))
